import numpy as np
import ml_dtypes


def mxq(x, axis, fmt="e4m3"):
    dtype, down = {"e4m3": (ml_dtypes.float8_e4m3fn, 7), "e5m2": (ml_dtypes.float8_e5m2, 14)}[fmt]
    v = np.moveaxis(np.asarray(x, np.float32).astype(ml_dtypes.bfloat16).astype(np.float64), axis, -1)
    blocks = v.reshape(v.shape[:-1] + (-1, 32))
    amax = np.abs(blocks).max(-1, keepdims=True)
    byte = np.maximum(np.where(amax > 0, np.frexp(amax)[1] - 1 + 127, 0) - down, 1)
    scale = np.exp2(byte - 127.0)
    codes = (blocks / scale).astype(np.float32).astype(dtype).astype(np.float64)
    return np.moveaxis((codes * scale).reshape(v.shape), -1, axis)


WIDE = False


def mx_kscale(k):
    if not WIDE:
        return np.ones(k)
    levels = np.array([10, -10, 5, -5, 0])
    a = np.random.permutation(np.resize(levels, k // 512 * 4)).reshape(k // 512, 4)
    idx = np.arange(k)
    return np.exp2(a[idx // 512, idx % 128 // 32])


BF16 = ml_dtypes.bfloat16


def bf(x):
    return np.asarray(x, np.float32).astype(BF16)


def f64(x):
    return np.asarray(x).astype(np.float64)


E2M1 = np.array([0.0, 0.5, 1.0, 1.5, 2.0, 3.0, 4.0, 6.0, -0.0, -0.5, -1.0, -1.5, -2.0, -3.0, -4.0, -6.0])


def pack_weight(w, fmt):
    k, n = w.shape
    w = f64(bf(w)).reshape(k // 32, 32, n)
    amax = np.abs(w).max(1)
    if fmt == "e4m3":
        byte = np.frexp(amax)[1] - 1 + 127 - 7
    else:
        mant, ex = np.frexp(amax / 6.0)
        byte = np.where(mant > 0.5, ex, ex - 1) + 127
    byte = np.clip(np.where(amax > 0, byte, 1), 1, 254)
    scaled = (w * np.exp2(127.0 - byte)[:, None, :]).reshape(k, n).astype(np.float32)
    by_word = np.ascontiguousarray(scaled.reshape(k // 512, 128, 4, n).transpose(0, 1, 3, 2))
    if fmt == "e4m3":
        words = by_word.astype(ml_dtypes.float8_e4m3fn).view(np.uint8)
    else:
        c = by_word.astype(ml_dtypes.float4_e2m1fn).view(np.uint8) & 0xF
        words = c[..., 0::2] | (c[..., 1::2] << 4)
    return np.ascontiguousarray(words), np.ascontiguousarray(byte.astype(np.uint8).reshape(k // 512, 16, n))


def unpack_weight(words, scales, fmt):
    g, p, n, _ = words.shape
    if fmt == "e4m3":
        vals = np.ascontiguousarray(words).view(ml_dtypes.float8_e4m3fn).astype(np.float64)
    else:
        nib = np.empty((g, p, n, 4), np.uint8)
        nib[..., 0::2] = words & 0xF
        nib[..., 1::2] = words >> 4
        vals = E2M1[nib]
    vals = vals * np.repeat(np.exp2(scales.astype(np.float64) - 127.0), 8, axis=1)[..., None]
    return vals.transpose(0, 1, 3, 2).reshape(g * 512, n)


B, NB, IBS, BS = 256, 8, 512, 512


def sigmoid(v):
    return 1.0 / (1.0 + np.exp(-v))


def setup_inputs():
    s = mx_kscale(IBS)
    x = bf((np.random.standard_normal((B, NB, IBS)) * s).reshape(B, NB * IBS))
    h = bf(np.random.standard_normal((B, NB * BS)))
    W_ih = np.random.standard_normal((NB, 3 * BS, IBS)) / np.sqrt(IBS) / s
    W_hh = np.random.standard_normal((NB, 3 * BS, BS)) / np.sqrt(BS)
    b_ih = bf(np.random.standard_normal((NB, 3 * BS)) * 0.2)
    b_hh = bf(np.random.standard_normal((NB, 3 * BS)) * 0.2)
    W_ih_words, W_ih_scales = pack_weight(np.ascontiguousarray(W_ih.swapaxes(1, 2)).reshape(-1, 3 * BS), "e4m3")
    W_hh_words, W_hh_scales = pack_weight(np.ascontiguousarray(W_hh.swapaxes(1, 2)).reshape(-1, 3 * BS), "e4m3")
    return {
        "x": x,
        "h": h,
        "W_ih_words": W_ih_words,
        "W_ih_scales": W_ih_scales,
        "W_hh_words": W_hh_words,
        "W_hh_scales": W_hh_scales,
        "b_ih": b_ih,
        "b_hh": b_hh,
    }


def reference(x, h, W_ih_words, W_ih_scales, W_hh_words, W_hh_scales, b_ih, b_hh):
    xb = f64(x).reshape(B, NB, IBS)
    hb = f64(h).reshape(B, NB, BS)
    gi = (mxq(xb, 2, "e4m3").transpose(1, 0, 2) @ unpack_weight(W_ih_words, W_ih_scales, "e4m3").reshape(NB, IBS, 3 * BS)).transpose(1, 0, 2) + f64(b_ih)
    gh = (mxq(hb, 2, "e4m3").transpose(1, 0, 2) @ unpack_weight(W_hh_words, W_hh_scales, "e4m3").reshape(NB, BS, 3 * BS)).transpose(1, 0, 2) + f64(b_hh)
    i_r, i_z, i_n = np.split(gi, 3, axis=-1)
    h_r, h_z, h_n = np.split(gh, 3, axis=-1)
    r = sigmoid(i_r + h_r)
    z = sigmoid(i_z + h_z)
    n_gate = np.tanh(i_n + r * h_n)
    new_h = n_gate + z * (hb - n_gate)
    return new_h.reshape(B, NB * BS)

@@ -1,0 +1,330 @@
+from contextlib import ExitStack
+
+import concourse.mybir as mybir
+from concourse.masks import make_identity
+
+F32 = mybir.dt.float32
+BF16 = mybir.dt.bfloat16
+I32 = mybir.dt.int32
+U32 = mybir.dt.uint32
+U8 = mybir.dt.uint8
+FP8X4 = mybir.dt.float8_e4m3fn_x4
+ALU = mybir.AluOpType
+ACT = mybir.ActivationFunctionType
+
+P = 128
+BATCH = 256
+HALVES = BATCH // P
+BLOCKS = 8
+K = 512
+HID = 512
+GATES = 3
+GATE_COLS = GATES * HID
+TILES = HID // P
+PAIR = 2
+UNITS = BLOCKS * TILES // PAIR
+UNITS_PER_BLOCK = TILES // PAIR
+UNIT_COLS = PAIR * P
+CHUNK_BLOCKS = 2
+PLANES = 4
+AHEAD = 4
+R, Z, N = 0, 1, 2
+
+FLOPS = 2 * BATCH * K * GATE_COLS * 2 * BLOCKS
+
+
+def tile_blockdiagonalgru_e_kernel(
+    tc, x, h, W_ih_words, W_ih_scales, W_hh_words, W_hh_scales, b_ih, b_hh, out
+):
+    nc = tc.nc
+    with ExitStack() as ctx:
+        ctx.enter_context(tc.manual_schedule())
+        keep = ctx.enter_context(tc.tile_pool(name="keep", bufs=1))
+        work = ctx.enter_context(tc.tile_pool(name="work", bufs=2))
+        psum = ctx.enter_context(tc.psum_pool(name="psum", bufs=1))
+
+        plane_tiles = []
+        for a in range(BLOCKS // PLANES):
+            planes = keep.tile([P, 2, GATE_COLS], U8, name="planes%d" % a, align_bytes=64)
+            nc.vector.memset(planes[:].rearrange("p m n -> p (m n)").bitcast(I32), 0)
+            plane_tiles.append(planes)
+
+        def load_planes(a):
+            for m, scales in enumerate((W_ih_scales, W_hh_scales)):
+                for quad in range(4):
+                    nc.sync.dma_start(
+                        out=plane_tiles[a][32 * quad : 32 * quad + 4 * PLANES, m, :].bitcast(I32),
+                        in_=scales[PLANES * a : PLANES * (a + 1), 4 * quad : 4 * quad + 4, :].bitcast(I32),
+                    )
+
+        act_tiles = ([], [])
+
+        def load_activations(c):
+            cols = slice(CHUNK_BLOCKS * K * c, CHUNK_BLOCKS * K * (c + 1))
+            for operand, src in enumerate((x, h)):
+                chunk = keep.tile([P, HALVES, CHUNK_BLOCKS * K], BF16, name="act%d_%d" % (operand, c))
+                nc.sync.dma_start(out=chunk[:], in_=src.rearrange("(b p) c -> p b c", p=P)[:, :, cols])
+                act_tiles[operand].append(chunk)
+
+        word_tiles = ([], [])
+
+        def load_words(g):
+            for m, words in enumerate((W_ih_words, W_hh_words)):
+                w = keep.tile([P, GATE_COLS], U32, name="w%d_%d" % (m, g), align_bytes=64)
+                nc.sync.dma_start(
+                    out=w[:].bitcast(I32), in_=words[g].rearrange("p n t -> p (n t)").bitcast(I32)
+                )
+                word_tiles[m].append(w)
+
+        load_activations(0)
+        load_planes(0)
+        for g in range(BLOCKS):
+            if g == PLANES:
+                load_planes(1)
+            load_words(g)
+            if g % CHUNK_BLOCKS == 0 and g // CHUNK_BLOCKS + 1 < BLOCKS // CHUNK_BLOCKS:
+                load_activations(g // CHUNK_BLOCKS + 1)
+
+        bias_rows = keep.tile([P, 2, P], BF16, name="bias_rows")
+        nc.vector.memset(bias_rows[:], 0.0)
+        runs = BLOCKS * GATES * TILES
+        for m, b in enumerate((b_ih, b_hh)):
+            nc.scalar.dma_start(out=bias_rows[0:runs, m, :], in_=b.rearrange("g (c q) -> (g c) q", q=P))
+
+        warm = keep.tile([P, 1], F32, name="warm")
+        nc.vector.memset(warm[:], 0.0)
+        nc.scalar.activation(out=warm[:], in_=warm[:], func=ACT.Sigmoid)
+
+        bias_rows32 = keep.tile([P, 2, P], F32, name="bias_rows32")
+        nc.vector.tensor_copy(out=bias_rows32[:], in_=bias_rows[:])
+
+        ident = keep.tile([P, P], F32, name="ident")
+        make_identity(nc, ident[:])
+
+        turn_banks = 4
+        turned = []
+
+        def turn_tile(shape, name):
+            t = psum.tile(shape, F32, name=name, tag="turn%d" % (len(turned) % turn_banks))
+            turned.append(name)
+            return t
+
+        bias = keep.tile([P, 2, P], F32, name="bias")
+        bias_sum = keep.tile([P, P], F32, name="bias_sum")
+        bias_neg = keep.tile([P, P], F32, name="bias_neg")
+        bias_ps = []
+
+        def transpose_biases():
+            ps = turn_tile([P, 2, P], "bias_ps")
+            for m in range(2):
+                nc.tensor.transpose(ps[:, m, :], bias_rows32[:, m, :], ident[:])
+            bias_ps.append(ps)
+
+        def finish_biases():
+            nc.vector.tensor_copy(out=bias[:], in_=bias_ps[0][:])
+            nc.vector.tensor_tensor(out=bias_sum[:], in0=bias[:, 0, :], in1=bias[:, 1, :], op=ALU.add)
+            nc.vector.tensor_scalar_mul(out=bias_neg[:], in0=bias_sum[:], scalar1=-1.0)
+
+        def bias_col(g, gate, j):
+            col = (g * GATES + gate) * TILES + j
+            return slice(col, col + 1)
+
+        part_ps = {}
+        grouped_tiles = {}
+        code_tiles = {}
+
+        def transpose_part(q):
+            g, operand = q // 2, q % 2
+            chunk = act_tiles[operand][g // CHUNK_BLOCKS]
+            first_word = (g % CHUNK_BLOCKS) * (K // 2)
+            ps = turn_tile([P, 2, HALVES, P], "part_ps%d" % q)
+            for u in range(2):
+                for b in range(HALVES):
+                    words = chunk[:, b, :].bitcast(F32)
+                    nc.tensor.transpose(
+                        ps[:, u, b, :], words[:, first_word + u : first_word + K // 2 : 2], ident[:]
+                    )
+            part_ps[q] = ps
+
+        def copy_part(q):
+            g, operand = q // 2, q % 2
+            if operand == 0:
+                grouped_tiles[g] = work.tile([P, 2, BATCH * 4], BF16, name="grouped%d" % g, tag="grouped", align_bytes=64)
+            nc.scalar.copy(
+                out=grouped_tiles[g][:, operand, :].bitcast(F32).rearrange("p (n u) -> p n u", u=2),
+                in_=part_ps[q][:].rearrange("p u b n -> p (b n) u"),
+            )
+
+        def quantise(g):
+            codes = work.tile([P, 2, BATCH], U32, name="codes%d" % g, tag="codes", bufs=3, align_bytes=64)
+            scales = work.tile([P, 2, BATCH], U8, name="scales%d" % g, tag="scales", bufs=3, align_bytes=64)
+            nc.vector.quantize_mx(
+                out=codes[:].rearrange("p o n -> p (o n)").bitcast(FP8X4),
+                scales=scales[:].rearrange("p o n -> p (o n)"),
+                in_=grouped_tiles[g][:].rearrange("p o n -> p (o n)"),
+            )
+            code_tiles[g] = (codes, scales)
+
+        def mx_pass(acc, g, m, gate, j, start, stop):
+            cols = slice(gate * HID + j * P, gate * HID + (j + 1) * P)
+            codes, scales = code_tiles[g]
+            offset = 4 * (g % PLANES)
+            nc.tensor.matmul_mx(
+                out=acc,
+                lhsT=word_tiles[m][g][:, cols].bitcast(FP8X4),
+                lhsT_scale=plane_tiles[g // PLANES][offset:P, m, cols],
+                rhs=codes[:, m, :].bitcast(FP8X4),
+                rhs_scale=scales[:, m, :],
+                start=start,
+                stop=stop,
+            )
+
+        sums = {}
+        gate_tiles = {}
+        back_ps = {}
+        out_tiles = [keep.tile([P, HALVES, HID], F32, name="new_h%d" % g) for g in range(BLOCKS)]
+
+        def column_tiles(s):
+            g = s // UNITS_PER_BLOCK
+            return g, [PAIR * (s % UNITS_PER_BLOCK) + i for i in range(PAIR)]
+
+        def multiply(s):
+            g, tiles = column_tiles(s)
+            acc = {}
+            for name in ("r", "hn", "in", "z"):
+                acc[name] = psum.tile([P, PAIR, BATCH], F32, name="%s_ps%d" % (name, s), tag=name)
+            for i, j in enumerate(tiles):
+                mx_pass(acc["r"][:, i, :], g, 0, R, j, True, False)
+                mx_pass(acc["r"][:, i, :], g, 1, R, j, False, True)
+            for i, j in enumerate(tiles):
+                mx_pass(acc["hn"][:, i, :], g, 1, N, j, True, True)
+            for i, j in enumerate(tiles):
+                mx_pass(acc["in"][:, i, :], g, 0, N, j, True, True)
+            for i, j in enumerate(tiles):
+                mx_pass(acc["z"][:, i, :], g, 0, Z, j, True, False)
+                mx_pass(acc["z"][:, i, :], g, 1, Z, j, False, True)
+            sums[s] = acc
+            gate_tiles[s] = {}
+            for name in ("r", "t", "zc", "c"):
+                gate_tiles[s][name] = work.tile([P, PAIR, BATCH], F32, name="%s%d" % (name, s), tag=name, bufs=3)
+
+        def reset_gate(s):
+            g, tiles = column_tiles(s)
+            for i, j in enumerate(tiles):
+                nc.scalar.activation(
+                    out=gate_tiles[s]["r"][:, i, :],
+                    in_=sums[s]["r"][:, i, :],
+                    func=ACT.Sigmoid,
+                    bias=bias_sum[:, bias_col(g, R, j)],
+                    scale=1.0,
+                )
+
+        def reset_times_hn(s):
+            g, tiles = column_tiles(s)
+            for i, j in enumerate(tiles):
+                nc.vector.scalar_tensor_tensor(
+                    out=gate_tiles[s]["t"][:, i, :],
+                    in0=sums[s]["hn"][:, i, :],
+                    scalar=bias[:, 1, bias_col(g, N, j)],
+                    in1=gate_tiles[s]["r"][:, i, :],
+                    op0=ALU.add,
+                    op1=ALU.mult,
+                )
+
+        def add_in(s):
+            t = gate_tiles[s]["t"]
+            nc.vector.tensor_tensor(out=t[:], in0=t[:], in1=sums[s]["in"][:], op=ALU.add)
+
+        def update_gate(s):
+            g, tiles = column_tiles(s)
+            for i, j in enumerate(tiles):
+                nc.scalar.activation(
+                    out=gate_tiles[s]["zc"][:, i, :],
+                    in_=sums[s]["z"][:, i, :],
+                    func=ACT.Sigmoid,
+                    bias=bias_neg[:, bias_col(g, Z, j)],
+                    scale=-1.0,
+                )
+
+        def candidate(s):
+            g, tiles = column_tiles(s)
+            for i, j in enumerate(tiles):
+                nc.scalar.activation(
+                    out=gate_tiles[s]["c"][:, i, :],
+                    in_=gate_tiles[s]["t"][:, i, :],
+                    func=ACT.Tanh,
+                    bias=bias[:, 0, bias_col(g, N, j)],
+                    scale=1.0,
+                )
+
+        def turn_back(s):
+            back_ps[s] = {}
+            for name in ("c", "zc"):
+                ps = turn_tile([P, HALVES, PAIR, P], "%s_back%d" % (name, s))
+                for b in range(HALVES):
+                    for i in range(PAIR):
+                        nc.tensor.transpose(
+                            ps[:, b, i, :], gate_tiles[s][name][:, i, b * P : (b + 1) * P], ident[:]
+                        )
+                back_ps[s][name] = ps
+
+        def blend_views(s):
+            g = s // UNITS_PER_BLOCK
+            first = (s % UNITS_PER_BLOCK) * UNIT_COLS
+            h_first = (g % CHUNK_BLOCKS) * K + first
+            h_view = act_tiles[1][g // CHUNK_BLOCKS][:, :, h_first : h_first + UNIT_COLS]
+            return h_view, out_tiles[g][:, :, first : first + UNIT_COLS]
+
+        def blend_difference(s):
+            h_view, o_view = blend_views(s)
+            c_view = back_ps[s]["c"][:].rearrange("p b i q -> p b (i q)")
+            nc.vector.tensor_tensor(out=o_view, in0=h_view, in1=c_view, op=ALU.subtract)
+
+        def blend_product(s):
+            h_view, o_view = blend_views(s)
+            zc_view = back_ps[s]["zc"][:].rearrange("p b i q -> p b (i q)")
+            nc.vector.tensor_tensor(out=o_view, in0=zc_view, in1=o_view, op=ALU.mult)
+
+        def blend_finish(s):
+            h_view, o_view = blend_views(s)
+            nc.gpsimd.tensor_tensor(out=o_view, in0=h_view, in1=o_view, op=ALU.subtract)
+
+        def store(g):
+            nc.sync.dma_start(
+                out=out.rearrange("(b p) c -> p b c", p=P)[:, :, g * HID : (g + 1) * HID], in_=out_tiles[g][:]
+            )
+
+        parts = 2 * BLOCKS
+        for q in range(AHEAD):
+            transpose_part(q)
+        transpose_biases()
+        for q in range(AHEAD):
+            copy_part(q)
+            if q % 2 == 1:
+                quantise(q // 2)
+        finish_biases()
+
+        for s in range(UNITS + 2):
+            if s < UNITS:
+                multiply(s)
+                reset_gate(s)
+                reset_times_hn(s)
+            if s + AHEAD < parts:
+                transpose_part(s + AHEAD)
+            if 1 <= s <= UNITS:
+                turn_back(s - 1)
+            if 1 <= s and s + AHEAD - 1 < parts:
+                copy_part(s + AHEAD - 1)
+            if s >= 2:
+                blend_difference(s - 2)
+            if s < UNITS:
+                add_in(s)
+                update_gate(s)
+                candidate(s)
+            if s >= 2:
+                blend_product(s - 2)
+                blend_finish(s - 2)
+                if (s - 2) % UNITS_PER_BLOCK == UNITS_PER_BLOCK - 1:
+                    store((s - 2) // UNITS_PER_BLOCK)
+            if 1 <= s and s + AHEAD - 1 < parts and (s + AHEAD - 1) % 2 == 1:
+                quantise((s + AHEAD - 1) // 2)

@@ -69,12 +69,18 @@ def tile_blockdiagonalgru_e_kernel(
         word_tiles = ([], [])
 
         def load_words(g):
-            for m, words in enumerate((W_ih_words, W_hh_words)):
-                w = keep.tile([P, GATE_COLS], U32, name="w%d_%d" % (m, g), align_bytes=64)
-                nc.sync.dma_start(
-                    out=w[:].bitcast(I32), in_=words[g].rearrange("p n t -> p (n t)").bitcast(I32)
-                )
-                word_tiles[m].append(w)
+            pieces = UNITS_PER_BLOCK if g == 0 else 1
+            split = "p (gate piece c) -> p gate piece c"
+            for m in range(2):
+                word_tiles[m].append(keep.tile([P, GATE_COLS], U32, name="w%d_%d" % (m, g), align_bytes=64))
+            for piece in range(pieces):
+                for m, words in enumerate((W_ih_words, W_hh_words)):
+                    sbuf_side = word_tiles[m][g][:].bitcast(I32)
+                    dram_side = words[g].rearrange("p n t -> p (n t)").bitcast(I32)
+                    nc.sync.dma_start(
+                        out=sbuf_side.rearrange(split, gate=GATES, piece=pieces)[:, :, piece, :],
+                        in_=dram_side.rearrange(split, gate=GATES, piece=pieces)[:, :, piece, :],
+                    )
 
         load_activations(0)
         load_planes(0)
@@ -182,7 +188,7 @@ def tile_blockdiagonalgru_e_kernel(
         sums = {}
         gate_tiles = {}
         back_ps = {}
-        out_tiles = [keep.tile([P, HALVES, HID], F32, name="new_h%d" % g) for g in range(BLOCKS)]
+        out_tiles = [keep.tile([P, HALVES, UNIT_COLS], F32, name="new_h%d" % s) for s in range(UNITS)]
 
         def column_tiles(s):
             g = s // UNITS_PER_BLOCK
@@ -259,7 +265,7 @@ def tile_blockdiagonalgru_e_kernel(
 
         def turn_back(s):
             back_ps[s] = {}
-            for name in ("c", "zc"):
+            for name in ("zc", "c"):
                 ps = turn_tile([P, HALVES, PAIR, P], "%s_back%d" % (name, s))
                 for b in range(HALVES):
                     for i in range(PAIR):
@@ -270,10 +276,9 @@ def tile_blockdiagonalgru_e_kernel(
 
         def blend_views(s):
             g = s // UNITS_PER_BLOCK
-            first = (s % UNITS_PER_BLOCK) * UNIT_COLS
-            h_first = (g % CHUNK_BLOCKS) * K + first
+            h_first = (g % CHUNK_BLOCKS) * K + (s % UNITS_PER_BLOCK) * UNIT_COLS
             h_view = act_tiles[1][g // CHUNK_BLOCKS][:, :, h_first : h_first + UNIT_COLS]
-            return h_view, out_tiles[g][:, :, first : first + UNIT_COLS]
+            return h_view, out_tiles[s][:]
 
         def blend_difference(s):
             h_view, o_view = blend_views(s)
@@ -287,12 +292,12 @@ def tile_blockdiagonalgru_e_kernel(
 
         def blend_finish(s):
             h_view, o_view = blend_views(s)
-            nc.gpsimd.tensor_tensor(out=o_view, in0=h_view, in1=o_view, op=ALU.subtract)
+            engine = nc.vector if s == UNITS - 1 else nc.gpsimd
+            engine.tensor_tensor(out=o_view, in0=h_view, in1=o_view, op=ALU.subtract)
 
-        def store(g):
-            nc.sync.dma_start(
-                out=out.rearrange("(b p) c -> p b c", p=P)[:, :, g * HID : (g + 1) * HID], in_=out_tiles[g][:]
-            )
+        def store(s):
+            cols = slice(s * UNIT_COLS, (s + 1) * UNIT_COLS)
+            nc.sync.dma_start(out=out.rearrange("(b p) c -> p b c", p=P)[:, :, cols], in_=out_tiles[s][:])
 
         parts = 2 * BLOCKS
         for q in range(AHEAD):
@@ -305,26 +310,28 @@ def tile_blockdiagonalgru_e_kernel(
         finish_biases()
 
         for s in range(UNITS + 2):
+            copied = s + AHEAD - 1
+            if 1 <= s and copied < parts:
+                copy_part(copied)
             if s < UNITS:
                 multiply(s)
+            if s >= 2:
+                blend_difference(s - 2)
+            if s < UNITS:
                 reset_gate(s)
                 reset_times_hn(s)
+            if 1 <= s <= UNITS:
+                candidate(s - 1)
             if s + AHEAD < parts:
                 transpose_part(s + AHEAD)
             if 1 <= s <= UNITS:
                 turn_back(s - 1)
-            if 1 <= s and s + AHEAD - 1 < parts:
-                copy_part(s + AHEAD - 1)
-            if s >= 2:
-                blend_difference(s - 2)
-            if s < UNITS:
-                add_in(s)
-                update_gate(s)
-                candidate(s)
             if s >= 2:
                 blend_product(s - 2)
                 blend_finish(s - 2)
-                if (s - 2) % UNITS_PER_BLOCK == UNITS_PER_BLOCK - 1:
-                    store((s - 2) // UNITS_PER_BLOCK)
-            if 1 <= s and s + AHEAD - 1 < parts and (s + AHEAD - 1) % 2 == 1:
-                quantise((s + AHEAD - 1) // 2)
+                store(s - 2)
+            if s < UNITS:
+                add_in(s)
+                update_gate(s)
+            if 1 <= s and copied < parts and copied % 2 == 1:
+                quantise(copied // 2)

@@ -25,12 +25,16 @@ PAIR = 2
 UNITS = BLOCKS * TILES // PAIR
 UNITS_PER_BLOCK = TILES // PAIR
 UNIT_COLS = PAIR * P
-CHUNK_BLOCKS = 2
+PARTS = 2 * BLOCKS
 PLANES = 4
-AHEAD = 4
+AHEAD = 3
 R, Z, N = 0, 1, 2
 
 FLOPS = 2 * BATCH * K * GATE_COLS * 2 * BLOCKS
+
+
+def parts_of_turn(s):
+    return [q for q in range(2, PARTS) if max(q - AHEAD, 0) == s]
 
 
 def tile_blockdiagonalgru_e_kernel(
@@ -57,105 +61,118 @@ def tile_blockdiagonalgru_e_kernel(
                         in_=scales[PLANES * a : PLANES * (a + 1), 4 * quad : 4 * quad + 4, :].bitcast(I32),
                     )
 
-        act_tiles = ([], [])
+        part_tiles = [keep.tile([P, HALVES, K], BF16, name="part%d" % q) for q in range(PARTS)]
 
-        def load_activations(c):
-            cols = slice(CHUNK_BLOCKS * K * c, CHUNK_BLOCKS * K * (c + 1))
-            for operand, src in enumerate((x, h)):
-                chunk = keep.tile([P, HALVES, CHUNK_BLOCKS * K], BF16, name="act%d_%d" % (operand, c))
-                nc.sync.dma_start(out=chunk[:], in_=src.rearrange("(b p) c -> p b c", p=P)[:, :, cols])
-                act_tiles[operand].append(chunk)
+        def load_part(q):
+            src = (x, h)[q % 2]
+            cols = slice(K * (q // 2), K * (q // 2 + 1))
+            nc.sync.dma_start(out=part_tiles[q][:], in_=src.rearrange("(b p) c -> p b c", p=P)[:, :, cols])
 
-        word_tiles = ([], [])
+        word_tiles = [
+            [keep.tile([P, GATE_COLS], U32, name="w%d_%d" % (m, g), align_bytes=64) for g in range(BLOCKS)]
+            for m in range(2)
+        ]
 
-        def load_words(g):
+        def load_words(s):
+            g, piece = s // UNITS_PER_BLOCK, s % UNITS_PER_BLOCK
             pieces = UNITS_PER_BLOCK if g == 0 else 1
+            if piece >= pieces:
+                return
             split = "p (gate piece c) -> p gate piece c"
-            for m in range(2):
-                word_tiles[m].append(keep.tile([P, GATE_COLS], U32, name="w%d_%d" % (m, g), align_bytes=64))
-            for piece in range(pieces):
-                for m, words in enumerate((W_ih_words, W_hh_words)):
-                    sbuf_side = word_tiles[m][g][:].bitcast(I32)
-                    dram_side = words[g].rearrange("p n t -> p (n t)").bitcast(I32)
-                    nc.sync.dma_start(
-                        out=sbuf_side.rearrange(split, gate=GATES, piece=pieces)[:, :, piece, :],
-                        in_=dram_side.rearrange(split, gate=GATES, piece=pieces)[:, :, piece, :],
-                    )
+            for m, words in enumerate((W_ih_words, W_hh_words)):
+                sbuf_side = word_tiles[m][g][:].bitcast(I32)
+                dram_side = words[g].rearrange("p n t -> p (n t)").bitcast(I32)
+                nc.sync.dma_start(
+                    out=sbuf_side.rearrange(split, gate=GATES, piece=pieces)[:, :, piece, :],
+                    in_=dram_side.rearrange(split, gate=GATES, piece=pieces)[:, :, piece, :],
+                )
 
-        load_activations(0)
+        load_part(0)
+        load_part(1)
         load_planes(0)
-        for g in range(BLOCKS):
-            if g == PLANES:
+        for s in range(UNITS):
+            if s == PLANES * UNITS_PER_BLOCK:
                 load_planes(1)
-            load_words(g)
-            if g % CHUNK_BLOCKS == 0 and g // CHUNK_BLOCKS + 1 < BLOCKS // CHUNK_BLOCKS:
-                load_activations(g // CHUNK_BLOCKS + 1)
+            load_words(s)
+            for q in parts_of_turn(s):
+                load_part(q)
 
         bias_rows = keep.tile([P, 2, P], BF16, name="bias_rows")
         nc.vector.memset(bias_rows[:], 0.0)
+        z_rows = keep.tile([P, HID], BF16, name="z_rows")
+        nc.vector.memset(z_rows[:], 0.0)
         runs = BLOCKS * GATES * TILES
         for m, b in enumerate((b_ih, b_hh)):
             nc.scalar.dma_start(out=bias_rows[0:runs, m, :], in_=b.rearrange("g (c q) -> (g c) q", q=P))
+            nc.scalar.dma_start(out=z_rows[m * BLOCKS : (m + 1) * BLOCKS, :], in_=b[:, Z * HID : (Z + 1) * HID])
 
         warm = keep.tile([P, 1], F32, name="warm")
         nc.vector.memset(warm[:], 0.0)
         nc.scalar.activation(out=warm[:], in_=warm[:], func=ACT.Sigmoid)
 
+        ident = keep.tile([P, P], F32, name="ident")
+        make_identity(nc, ident[:])
+        pick = keep.tile([P, BLOCKS], BF16, name="pick")
+        nc.vector.tensor_tensor(out=pick[:], in0=ident[:, 0:BLOCKS], in1=ident[:, BLOCKS : 2 * BLOCKS], op=ALU.add)
+
         bias_rows32 = keep.tile([P, 2, P], F32, name="bias_rows32")
         nc.vector.tensor_copy(out=bias_rows32[:], in_=bias_rows[:])
 
-        ident = keep.tile([P, P], F32, name="ident")
-        make_identity(nc, ident[:])
+        spare_banks = 4
+        spare_names = []
 
-        turn_banks = 4
-        turned = []
-
-        def turn_tile(shape, name):
-            t = psum.tile(shape, F32, name=name, tag="turn%d" % (len(turned) % turn_banks))
-            turned.append(name)
+        def spare_tile(shape, name):
+            t = psum.tile(shape, F32, name=name, tag="spare%d" % (len(spare_names) % spare_banks))
+            spare_names.append(name)
             return t
 
         bias = keep.tile([P, 2, P], F32, name="bias")
         bias_sum = keep.tile([P, P], F32, name="bias_sum")
-        bias_neg = keep.tile([P, P], F32, name="bias_neg")
-        bias_ps = []
+        bias_ps = {}
 
         def transpose_biases():
-            ps = turn_tile([P, 2, P], "bias_ps")
+            bias_ps[0] = spare_tile([P, 2, P], "bias_ps")
             for m in range(2):
-                nc.tensor.transpose(ps[:, m, :], bias_rows32[:, m, :], ident[:])
-            bias_ps.append(ps)
+                nc.tensor.transpose(bias_ps[0][:, m, :], bias_rows32[:, m, :], ident[:])
 
         def finish_biases():
             nc.vector.tensor_copy(out=bias[:], in_=bias_ps[0][:])
             nc.vector.tensor_tensor(out=bias_sum[:], in0=bias[:, 0, :], in1=bias[:, 1, :], op=ALU.add)
-            nc.vector.tensor_scalar_mul(out=bias_neg[:], in0=bias_sum[:], scalar1=-1.0)
 
         def bias_col(g, gate, j):
             col = (g * GATES + gate) * TILES + j
             return slice(col, col + 1)
+
+        z_bias = keep.tile([P, BLOCKS, HID], F32, name="z_bias")
+        z_bias_ps = {}
+
+        def spread_z_bias(g):
+            z_bias_ps[g] = spare_tile([P, HID], "z_bias_ps%d" % g)
+            nc.tensor.matmul(
+                out=z_bias_ps[g][:], lhsT=pick[:, g : g + 1].to_broadcast([P, P]), rhs=z_rows[:], start=True, stop=True
+            )
+
+        def copy_z_bias(g):
+            nc.scalar.copy(out=z_bias[:, g, :], in_=z_bias_ps[g][:])
 
         part_ps = {}
         grouped_tiles = {}
         code_tiles = {}
 
         def transpose_part(q):
-            g, operand = q // 2, q % 2
-            chunk = act_tiles[operand][g // CHUNK_BLOCKS]
-            first_word = (g % CHUNK_BLOCKS) * (K // 2)
-            ps = turn_tile([P, 2, HALVES, P], "part_ps%d" % q)
+            ps = spare_tile([P, 2, HALVES, P], "part_ps%d" % q)
             for u in range(2):
                 for b in range(HALVES):
-                    words = chunk[:, b, :].bitcast(F32)
-                    nc.tensor.transpose(
-                        ps[:, u, b, :], words[:, first_word + u : first_word + K // 2 : 2], ident[:]
-                    )
+                    words = part_tiles[q][:, b, :].bitcast(F32)
+                    nc.tensor.transpose(ps[:, u, b, :], words[:, u : K // 2 : 2], ident[:])
             part_ps[q] = ps
 
         def copy_part(q):
             g, operand = q // 2, q % 2
             if operand == 0:
-                grouped_tiles[g] = work.tile([P, 2, BATCH * 4], BF16, name="grouped%d" % g, tag="grouped", align_bytes=64)
+                grouped_tiles[g] = work.tile(
+                    [P, 2, BATCH * 4], BF16, name="grouped%d" % g, tag="grouped", align_bytes=64
+                )
             nc.scalar.copy(
                 out=grouped_tiles[g][:, operand, :].bitcast(F32).rearrange("p (n u) -> p n u", u=2),
                 in_=part_ps[q][:].rearrange("p u b n -> p (b n) u"),
@@ -171,19 +188,23 @@ def tile_blockdiagonalgru_e_kernel(
             )
             code_tiles[g] = (codes, scales)
 
-        def mx_pass(acc, g, m, gate, j, start, stop):
-            cols = slice(gate * HID + j * P, gate * HID + (j + 1) * P)
-            codes, scales = code_tiles[g]
+        def weights(g, m, cols):
             offset = 4 * (g % PLANES)
-            nc.tensor.matmul_mx(
-                out=acc,
-                lhsT=word_tiles[m][g][:, cols].bitcast(FP8X4),
-                lhsT_scale=plane_tiles[g // PLANES][offset:P, m, cols],
-                rhs=codes[:, m, :].bitcast(FP8X4),
-                rhs_scale=scales[:, m, :],
-                start=start,
-                stop=stop,
-            )
+            return word_tiles[m][g][:, cols].bitcast(FP8X4), plane_tiles[g // PLANES][offset:P, m, cols]
+
+        def activations(g, m, rows):
+            codes, scales = code_tiles[g]
+            return codes[:, m, rows].bitcast(FP8X4), scales[:, m, rows]
+
+        def columns_by_batch(acc, g, m, gate, j, start, stop):
+            w, w_scale = weights(g, m, slice(gate * HID + j * P, gate * HID + (j + 1) * P))
+            a, a_scale = activations(g, m, slice(0, BATCH))
+            nc.tensor.matmul_mx(out=acc, lhsT=w, lhsT_scale=w_scale, rhs=a, rhs_scale=a_scale, start=start, stop=stop)
+
+        def batch_by_columns(acc, g, m, gate, first, b, start, stop):
+            w, w_scale = weights(g, m, slice(gate * HID + first, gate * HID + first + UNIT_COLS))
+            a, a_scale = activations(g, m, slice(b * P, (b + 1) * P))
+            nc.tensor.matmul_mx(out=acc, lhsT=a, lhsT_scale=a_scale, rhs=w, rhs_scale=w_scale, start=start, stop=stop)
 
         sums = {}
         gate_tiles = {}
@@ -197,22 +218,22 @@ def tile_blockdiagonalgru_e_kernel(
         def multiply(s):
             g, tiles = column_tiles(s)
             acc = {}
-            for name in ("r", "hn", "in", "z"):
+            for name in ("r", "hn", "z", "in"):
                 acc[name] = psum.tile([P, PAIR, BATCH], F32, name="%s_ps%d" % (name, s), tag=name)
             for i, j in enumerate(tiles):
-                mx_pass(acc["r"][:, i, :], g, 0, R, j, True, False)
-                mx_pass(acc["r"][:, i, :], g, 1, R, j, False, True)
+                columns_by_batch(acc["r"][:, i, :], g, 0, R, j, True, False)
+                columns_by_batch(acc["r"][:, i, :], g, 1, R, j, False, True)
             for i, j in enumerate(tiles):
-                mx_pass(acc["hn"][:, i, :], g, 1, N, j, True, True)
+                columns_by_batch(acc["hn"][:, i, :], g, 1, N, j, True, True)
+            for b in range(HALVES):
+                batch_by_columns(acc["z"][:, b, :], g, 0, Z, tiles[0] * P, b, True, False)
+                batch_by_columns(acc["z"][:, b, :], g, 1, Z, tiles[0] * P, b, False, True)
             for i, j in enumerate(tiles):
-                mx_pass(acc["in"][:, i, :], g, 0, N, j, True, True)
-            for i, j in enumerate(tiles):
-                mx_pass(acc["z"][:, i, :], g, 0, Z, j, True, False)
-                mx_pass(acc["z"][:, i, :], g, 1, Z, j, False, True)
+                columns_by_batch(acc["in"][:, i, :], g, 0, N, j, True, True)
             sums[s] = acc
             gate_tiles[s] = {}
-            for name in ("r", "t", "zc", "c"):
-                gate_tiles[s][name] = work.tile([P, PAIR, BATCH], F32, name="%s%d" % (name, s), tag=name, bufs=3)
+            for name, bufs in (("r", 2), ("t", 3), ("c", 2), ("zc", 4)):
+                gate_tiles[s][name] = work.tile([P, PAIR, BATCH], F32, name="%s%d" % (name, s), tag=name, bufs=bufs)
 
         def reset_gate(s):
             g, tiles = column_tiles(s)
@@ -241,16 +262,16 @@ def tile_blockdiagonalgru_e_kernel(
             t = gate_tiles[s]["t"]
             nc.vector.tensor_tensor(out=t[:], in0=t[:], in1=sums[s]["in"][:], op=ALU.add)
 
-        def update_gate(s):
+        def add_z_bias(s):
             g, tiles = column_tiles(s)
-            for i, j in enumerate(tiles):
-                nc.scalar.activation(
-                    out=gate_tiles[s]["zc"][:, i, :],
-                    in_=sums[s]["z"][:, i, :],
-                    func=ACT.Sigmoid,
-                    bias=bias_neg[:, bias_col(g, Z, j)],
-                    scale=-1.0,
-                )
+            both_halves = z_bias[:, g, tiles[0] * P : tiles[0] * P + UNIT_COLS].unsqueeze(1).to_broadcast(
+                [P, HALVES, UNIT_COLS]
+            )
+            nc.vector.tensor_tensor(out=gate_tiles[s]["zc"][:], in0=sums[s]["z"][:], in1=both_halves, op=ALU.add)
+
+        def update_gate(s):
+            zc = gate_tiles[s]["zc"]
+            nc.scalar.activation(out=zc[:], in_=zc[:], func=ACT.Sigmoid, scale=-1.0)
 
         def candidate(s):
             g, tiles = column_tiles(s)
@@ -264,74 +285,69 @@ def tile_blockdiagonalgru_e_kernel(
                 )
 
         def turn_back(s):
-            back_ps[s] = {}
-            for name in ("zc", "c"):
-                ps = turn_tile([P, HALVES, PAIR, P], "%s_back%d" % (name, s))
-                for b in range(HALVES):
-                    for i in range(PAIR):
-                        nc.tensor.transpose(
-                            ps[:, b, i, :], gate_tiles[s][name][:, i, b * P : (b + 1) * P], ident[:]
-                        )
-                back_ps[s][name] = ps
+            ps = spare_tile([P, HALVES, PAIR, P], "c_back%d" % s)
+            for b in range(HALVES):
+                for i in range(PAIR):
+                    nc.tensor.transpose(ps[:, b, i, :], gate_tiles[s]["c"][:, i, b * P : (b + 1) * P], ident[:])
+            back_ps[s] = ps
 
-        def blend_views(s):
-            g = s // UNITS_PER_BLOCK
-            h_first = (g % CHUNK_BLOCKS) * K + (s % UNITS_PER_BLOCK) * UNIT_COLS
-            h_view = act_tiles[1][g // CHUNK_BLOCKS][:, :, h_first : h_first + UNIT_COLS]
-            return h_view, out_tiles[s][:]
+        def h_columns(s):
+            first = (s % UNITS_PER_BLOCK) * UNIT_COLS
+            return part_tiles[2 * (s // UNITS_PER_BLOCK) + 1][:, :, first : first + UNIT_COLS]
 
         def blend_difference(s):
-            h_view, o_view = blend_views(s)
-            c_view = back_ps[s]["c"][:].rearrange("p b i q -> p b (i q)")
-            nc.vector.tensor_tensor(out=o_view, in0=h_view, in1=c_view, op=ALU.subtract)
-
-        def blend_product(s):
-            h_view, o_view = blend_views(s)
-            zc_view = back_ps[s]["zc"][:].rearrange("p b i q -> p b (i q)")
-            nc.vector.tensor_tensor(out=o_view, in0=zc_view, in1=o_view, op=ALU.mult)
+            c_view = back_ps[s][:].rearrange("p b i q -> p b (i q)")
+            nc.vector.tensor_tensor(out=out_tiles[s][:], in0=h_columns(s), in1=c_view, op=ALU.subtract)
 
         def blend_finish(s):
-            h_view, o_view = blend_views(s)
             engine = nc.vector if s == UNITS - 1 else nc.gpsimd
-            engine.tensor_tensor(out=o_view, in0=h_view, in1=o_view, op=ALU.subtract)
+            o = out_tiles[s]
+            engine.tensor_tensor(out=o[:], in0=gate_tiles[s]["zc"][:], in1=o[:], op=ALU.mult)
+            engine.tensor_tensor(out=o[:], in0=h_columns(s), in1=o[:], op=ALU.subtract)
 
         def store(s):
             cols = slice(s * UNIT_COLS, (s + 1) * UNIT_COLS)
             nc.sync.dma_start(out=out.rearrange("(b p) c -> p b c", p=P)[:, :, cols], in_=out_tiles[s][:])
 
-        parts = 2 * BLOCKS
-        for q in range(AHEAD):
-            transpose_part(q)
+        transpose_part(0)
+        transpose_part(1)
         transpose_biases()
-        for q in range(AHEAD):
-            copy_part(q)
-            if q % 2 == 1:
-                quantise(q // 2)
+        spread_z_bias(0)
+        copy_part(0)
+        copy_part(1)
+        quantise(0)
+        copy_z_bias(0)
         finish_biases()
 
         for s in range(UNITS + 2):
-            copied = s + AHEAD - 1
-            if 1 <= s and copied < parts:
-                copy_part(copied)
+            first_of_block = s % UNITS_PER_BLOCK == 0
+            next_block = s // UNITS_PER_BLOCK + 1
+            for q in parts_of_turn(s - 1):
+                copy_part(q)
+            if not first_of_block and next_block < BLOCKS:
+                copy_z_bias(next_block)
             if s < UNITS:
                 multiply(s)
             if s >= 2:
                 blend_difference(s - 2)
+            for q in parts_of_turn(s - 1):
+                if q % 2 == 1:
+                    quantise(q // 2)
             if s < UNITS:
                 reset_gate(s)
                 reset_times_hn(s)
             if 1 <= s <= UNITS:
                 candidate(s - 1)
-            if s + AHEAD < parts:
-                transpose_part(s + AHEAD)
+                update_gate(s - 1)
+            if first_of_block and next_block < BLOCKS:
+                spread_z_bias(next_block)
+            for q in parts_of_turn(s):
+                transpose_part(q)
             if 1 <= s <= UNITS:
                 turn_back(s - 1)
+            if s < UNITS:
+                add_z_bias(s)
+                add_in(s)
             if s >= 2:
-                blend_product(s - 2)
                 blend_finish(s - 2)
                 store(s - 2)
-            if s < UNITS:
-                add_in(s)
-                update_gate(s)
-            if 1 <= s and copied < parts and copied % 2 == 1:
-                quantise(copied // 2)

@@ -29,6 +29,7 @@ PARTS = 2 * BLOCKS
 PLANES = 4
 AHEAD = 3
 R, Z, N = 0, 1, 2
+SUMS = ("r", "hn", "z", "in")
 
 FLOPS = 2 * BATCH * K * GATE_COLS * 2 * BLOCKS
 
@@ -147,13 +148,16 @@ def tile_blockdiagonalgru_e_kernel(
         z_bias_ps = {}
 
         def spread_z_bias(g):
-            z_bias_ps[g] = spare_tile([P, HID], "z_bias_ps%d" % g)
+            z_bias_ps[g] = psum.tile([P, HID], F32, name="z_bias_ps%d" % g, tag=SUMS[g % len(SUMS)])
             nc.tensor.matmul(
                 out=z_bias_ps[g][:], lhsT=pick[:, g : g + 1].to_broadcast([P, P]), rhs=z_rows[:], start=True, stop=True
             )
 
         def copy_z_bias(g):
-            nc.scalar.copy(out=z_bias[:, g, :], in_=z_bias_ps[g][:])
+            if g % 2 == 0:
+                nc.scalar.copy(out=z_bias[:, g, :], in_=z_bias_ps[g][:])
+            else:
+                nc.vector.tensor_copy(out=z_bias[:, g, :], in_=z_bias_ps[g][:])
 
         part_ps = {}
         grouped_tiles = {}
@@ -218,7 +222,7 @@ def tile_blockdiagonalgru_e_kernel(
         def multiply(s):
             g, tiles = column_tiles(s)
             acc = {}
-            for name in ("r", "hn", "z", "in"):
+            for name in SUMS:
                 acc[name] = psum.tile([P, PAIR, BATCH], F32, name="%s_ps%d" % (name, s), tag=name)
             for i, j in enumerate(tiles):
                 columns_by_batch(acc["r"][:, i, :], g, 0, R, j, True, False)
@@ -312,20 +316,18 @@ def tile_blockdiagonalgru_e_kernel(
         transpose_part(0)
         transpose_part(1)
         transpose_biases()
-        spread_z_bias(0)
+        for g in range(BLOCKS):
+            spread_z_bias(g)
         copy_part(0)
         copy_part(1)
         quantise(0)
-        copy_z_bias(0)
         finish_biases()
+        for g in range(BLOCKS):
+            copy_z_bias(g)
 
         for s in range(UNITS + 2):
-            first_of_block = s % UNITS_PER_BLOCK == 0
-            next_block = s // UNITS_PER_BLOCK + 1
             for q in parts_of_turn(s - 1):
                 copy_part(q)
-            if not first_of_block and next_block < BLOCKS:
-                copy_z_bias(next_block)
             if s < UNITS:
                 multiply(s)
             if s >= 2:
@@ -339,8 +341,6 @@ def tile_blockdiagonalgru_e_kernel(
             if 1 <= s <= UNITS:
                 candidate(s - 1)
                 update_gate(s - 1)
-            if first_of_block and next_block < BLOCKS:
-                spread_z_bias(next_block)
             for q in parts_of_turn(s):
                 transpose_part(q)
             if 1 <= s <= UNITS:

@@ -48,6 +48,11 @@ def tile_blockdiagonalgru_e_kernel(
         work = ctx.enter_context(tc.tile_pool(name="work", bufs=2))
         psum = ctx.enter_context(tc.psum_pool(name="psum", bufs=1))
 
+        z_rows = keep.tile([P, HID], BF16, name="z_rows")
+        nc.vector.memset(z_rows[:], 0.0)
+        for m, b in enumerate((b_ih, b_hh)):
+            nc.scalar.dma_start(out=z_rows[m * BLOCKS : (m + 1) * BLOCKS, :], in_=b[:, Z * HID : (Z + 1) * HID])
+
         plane_tiles = []
         for a in range(BLOCKS // PLANES):
             planes = keep.tile([P, 2, GATE_COLS], U8, name="planes%d" % a, align_bytes=64)
@@ -100,12 +105,9 @@ def tile_blockdiagonalgru_e_kernel(
 
         bias_rows = keep.tile([P, 2, P], BF16, name="bias_rows")
         nc.vector.memset(bias_rows[:], 0.0)
-        z_rows = keep.tile([P, HID], BF16, name="z_rows")
-        nc.vector.memset(z_rows[:], 0.0)
         runs = BLOCKS * GATES * TILES
         for m, b in enumerate((b_ih, b_hh)):
             nc.scalar.dma_start(out=bias_rows[0:runs, m, :], in_=b.rearrange("g (c q) -> (g c) q", q=P))
-            nc.scalar.dma_start(out=z_rows[m * BLOCKS : (m + 1) * BLOCKS, :], in_=b[:, Z * HID : (Z + 1) * HID])
 
         warm = keep.tile([P, 1], F32, name="warm")
         nc.vector.memset(warm[:], 0.0)
@@ -313,16 +315,20 @@ def tile_blockdiagonalgru_e_kernel(
             cols = slice(s * UNIT_COLS, (s + 1) * UNIT_COLS)
             nc.sync.dma_start(out=out.rearrange("(b p) c -> p b c", p=P)[:, :, cols], in_=out_tiles[s][:])
 
+        for g in range(len(SUMS)):
+            spread_z_bias(g)
+        for g in range(len(SUMS)):
+            copy_z_bias(g)
         transpose_part(0)
         transpose_part(1)
         transpose_biases()
-        for g in range(BLOCKS):
-            spread_z_bias(g)
         copy_part(0)
         copy_part(1)
         quantise(0)
         finish_biases()
-        for g in range(BLOCKS):
+        for g in range(len(SUMS), BLOCKS):
+            spread_z_bias(g)
+        for g in range(len(SUMS), BLOCKS):
             copy_z_bias(g)
 
         for s in range(UNITS + 2):

@@ -42,25 +42,34 @@ def tile_blockdiagonalgru_e_kernel(
     tc, x, h, W_ih_words, W_ih_scales, W_hh_words, W_hh_scales, b_ih, b_hh, out
 ):
     nc = tc.nc
+    small_queue = nc.gpsimd
     with ExitStack() as ctx:
         ctx.enter_context(tc.manual_schedule())
         keep = ctx.enter_context(tc.tile_pool(name="keep", bufs=1))
         work = ctx.enter_context(tc.tile_pool(name="work", bufs=2))
         psum = ctx.enter_context(tc.psum_pool(name="psum", bufs=1))
 
+        warm = keep.tile([P, 1], F32, name="warm")
+        nc.gpsimd.memset(warm[:], 0.0)
+        nc.scalar.activation(out=warm[:], in_=warm[:], func=ACT.Sigmoid)
+
+        ident = keep.tile([P, P], F32, name="ident")
+        make_identity(nc, ident[:])
+
         z_rows = keep.tile([P, HID], BF16, name="z_rows")
-        nc.vector.memset(z_rows[:], 0.0)
-        for m, b in enumerate((b_ih, b_hh)):
-            nc.scalar.dma_start(out=z_rows[m * BLOCKS : (m + 1) * BLOCKS, :], in_=b[:, Z * HID : (Z + 1) * HID])
+        bias_rows = keep.tile([P, 2, P], BF16, name="bias_rows")
 
         plane_tiles = []
         for a in range(BLOCKS // PLANES):
             planes = keep.tile([P, 2, GATE_COLS], U8, name="planes%d" % a, align_bytes=64)
-            nc.vector.memset(planes[:].rearrange("p m n -> p (m n)").bitcast(I32), 0)
             plane_tiles.append(planes)
+        nc.vector.memset(bias_rows[:], 0.0)
+        nc.vector.memset(plane_tiles[0][:].rearrange("p m n -> p (m n)").bitcast(I32), 0)
+        nc.vector.memset(z_rows[:], 0.0)
+        nc.vector.memset(plane_tiles[1][:].rearrange("p m n -> p (m n)").bitcast(I32), 0)
 
-        def load_planes(a):
-            for m, scales in enumerate((W_ih_scales, W_hh_scales)):
+        def load_planes(a, m):
+            for scales in ((W_ih_scales, W_hh_scales)[m],):
                 for quad in range(4):
                     nc.sync.dma_start(
                         out=plane_tiles[a][32 * quad : 32 * quad + 4 * PLANES, m, :].bitcast(I32),
@@ -93,33 +102,30 @@ def tile_blockdiagonalgru_e_kernel(
                     in_=dram_side.rearrange(split, gate=GATES, piece=pieces)[:, :, piece, :],
                 )
 
+        runs = BLOCKS * GATES * TILES
+        for m, b in enumerate((b_ih, b_hh)):
+            small_queue.dma_start(out=bias_rows[0:runs, m, :], in_=b.rearrange("g (c q) -> (g c) q", q=P))
+        for m, b in enumerate((b_ih, b_hh)):
+            small_queue.dma_start(out=z_rows[m * BLOCKS : (m + 1) * BLOCKS, :], in_=b[:, Z * HID : (Z + 1) * HID])
+        load_planes(0, 0)
         load_part(0)
         load_part(1)
-        load_planes(0)
+        load_words(0)
+        load_planes(0, 1)
+        load_words(1)
         for s in range(UNITS):
             if s == PLANES * UNITS_PER_BLOCK:
-                load_planes(1)
-            load_words(s)
+                load_planes(1, 0)
+                load_planes(1, 1)
+            if s > 1:
+                load_words(s)
             for q in parts_of_turn(s):
                 load_part(q)
 
-        bias_rows = keep.tile([P, 2, P], BF16, name="bias_rows")
-        nc.vector.memset(bias_rows[:], 0.0)
-        runs = BLOCKS * GATES * TILES
-        for m, b in enumerate((b_ih, b_hh)):
-            nc.scalar.dma_start(out=bias_rows[0:runs, m, :], in_=b.rearrange("g (c q) -> (g c) q", q=P))
-
-        warm = keep.tile([P, 1], F32, name="warm")
-        nc.vector.memset(warm[:], 0.0)
-        nc.scalar.activation(out=warm[:], in_=warm[:], func=ACT.Sigmoid)
-
-        ident = keep.tile([P, P], F32, name="ident")
-        make_identity(nc, ident[:])
         pick = keep.tile([P, BLOCKS], BF16, name="pick")
         nc.vector.tensor_tensor(out=pick[:], in0=ident[:, 0:BLOCKS], in1=ident[:, BLOCKS : 2 * BLOCKS], op=ALU.add)
 
         bias_rows32 = keep.tile([P, 2, P], F32, name="bias_rows32")
-        nc.vector.tensor_copy(out=bias_rows32[:], in_=bias_rows[:])
 
         spare_banks = 4
         spare_names = []
@@ -150,13 +156,13 @@ def tile_blockdiagonalgru_e_kernel(
         z_bias_ps = {}
 
         def spread_z_bias(g):
-            z_bias_ps[g] = psum.tile([P, HID], F32, name="z_bias_ps%d" % g, tag=SUMS[g % len(SUMS)])
+            z_bias_ps[g] = spare_tile([P, HID], "z_bias_ps%d" % g)
             nc.tensor.matmul(
                 out=z_bias_ps[g][:], lhsT=pick[:, g : g + 1].to_broadcast([P, P]), rhs=z_rows[:], start=True, stop=True
             )
 
         def copy_z_bias(g):
-            if g % 2 == 0:
+            if g > 0:
                 nc.scalar.copy(out=z_bias[:, g, :], in_=z_bias_ps[g][:])
             else:
                 nc.vector.tensor_copy(out=z_bias[:, g, :], in_=z_bias_ps[g][:])
@@ -184,15 +190,22 @@ def tile_blockdiagonalgru_e_kernel(
                 in_=part_ps[q][:].rearrange("p u b n -> p (b n) u"),
             )
 
-        def quantise(g):
-            codes = work.tile([P, 2, BATCH], U32, name="codes%d" % g, tag="codes", bufs=3, align_bytes=64)
-            scales = work.tile([P, 2, BATCH], U8, name="scales%d" % g, tag="scales", bufs=3, align_bytes=64)
-            nc.vector.quantize_mx(
-                out=codes[:].rearrange("p o n -> p (o n)").bitcast(FP8X4),
-                scales=scales[:].rearrange("p o n -> p (o n)"),
-                in_=grouped_tiles[g][:].rearrange("p o n -> p (o n)"),
-            )
-            code_tiles[g] = (codes, scales)
+        def quantise(g, operand=None):
+            if operand != 1:
+                codes = work.tile([P, 2, BATCH], U32, name="codes%d" % g, tag="codes", bufs=3, align_bytes=64)
+                scales = work.tile([P, 2, BATCH], U8, name="scales%d" % g, tag="scales", bufs=3, align_bytes=64)
+                code_tiles[g] = (codes, scales)
+            codes, scales = code_tiles[g]
+            if operand is None:
+                nc.vector.quantize_mx(
+                    out=codes[:].rearrange("p o n -> p (o n)").bitcast(FP8X4),
+                    scales=scales[:].rearrange("p o n -> p (o n)"),
+                    in_=grouped_tiles[g][:].rearrange("p o n -> p (o n)"),
+                )
+            else:
+                nc.vector.quantize_mx(
+                    out=codes[:, operand, :].bitcast(FP8X4), scales=scales[:, operand, :], in_=grouped_tiles[g][:, operand, :]
+                )
 
         def weights(g, m, cols):
             offset = 4 * (g % PLANES)
@@ -306,36 +319,46 @@ def tile_blockdiagonalgru_e_kernel(
             nc.vector.tensor_tensor(out=out_tiles[s][:], in0=h_columns(s), in1=c_view, op=ALU.subtract)
 
         def blend_finish(s):
-            engine = nc.vector if s == UNITS - 1 else nc.gpsimd
             o = out_tiles[s]
-            engine.tensor_tensor(out=o[:], in0=gate_tiles[s]["zc"][:], in1=o[:], op=ALU.mult)
-            engine.tensor_tensor(out=o[:], in0=h_columns(s), in1=o[:], op=ALU.subtract)
+            nc.gpsimd.tensor_tensor(out=o[:], in0=gate_tiles[s]["zc"][:], in1=o[:], op=ALU.mult)
+            nc.gpsimd.tensor_tensor(out=o[:], in0=h_columns(s), in1=o[:], op=ALU.subtract)
+
+        def blend_step(s, b, step, engine):
+            o = out_tiles[s][:, b, :]
+            if step == 0:
+                engine.tensor_tensor(out=o, in0=gate_tiles[s]["zc"][:, b, :], in1=o, op=ALU.mult)
+            else:
+                engine.tensor_tensor(out=o, in0=h_columns(s)[:, b, :], in1=o, op=ALU.subtract)
+
+        def blend_finish_half(s, b, engine):
+            for step in range(2):
+                blend_step(s, b, step, engine)
 
         def store(s):
             cols = slice(s * UNIT_COLS, (s + 1) * UNIT_COLS)
             nc.sync.dma_start(out=out.rearrange("(b p) c -> p b c", p=P)[:, :, cols], in_=out_tiles[s][:])
 
-        for g in range(len(SUMS)):
-            spread_z_bias(g)
-        for g in range(len(SUMS)):
-            copy_z_bias(g)
+        def store_half(s, b):
+            cols = slice(s * UNIT_COLS, (s + 1) * UNIT_COLS)
+            nc.sync.dma_start(out=out[b * P : (b + 1) * P, cols], in_=out_tiles[s][:, b, :])
+
         transpose_part(0)
         transpose_part(1)
-        transpose_biases()
         copy_part(0)
+        quantise(0, 0)
         copy_part(1)
-        quantise(0)
+        quantise(0, 1)
+        nc.vector.tensor_copy(out=bias_rows32[:], in_=bias_rows[:])
+        transpose_biases()
         finish_biases()
-        for g in range(len(SUMS), BLOCKS):
-            spread_z_bias(g)
-        for g in range(len(SUMS), BLOCKS):
-            copy_z_bias(g)
 
         for s in range(UNITS + 2):
             for q in parts_of_turn(s - 1):
                 copy_part(q)
             if s < UNITS:
                 multiply(s)
+            if s == 0:
+                spread_z_bias(0)
             if s >= 2:
                 blend_difference(s - 2)
             for q in parts_of_turn(s - 1):
@@ -347,13 +370,29 @@ def tile_blockdiagonalgru_e_kernel(
             if 1 <= s <= UNITS:
                 candidate(s - 1)
                 update_gate(s - 1)
+            if s % 2 == 1 and (s + 1) // 2 < BLOCKS:
+                copy_z_bias((s + 1) // 2)
             for q in parts_of_turn(s):
                 transpose_part(q)
+            if s % 2 == 0 and s // 2 + 1 < BLOCKS:
+                spread_z_bias(s // 2 + 1)
             if 1 <= s <= UNITS:
                 turn_back(s - 1)
+            if s == 0:
+                copy_z_bias(0)
             if s < UNITS:
                 add_z_bias(s)
                 add_in(s)
-            if s >= 2:
+            if 2 <= s < UNITS:
                 blend_finish(s - 2)
                 store(s - 2)
+            if s == UNITS:
+                blend_finish_half(UNITS - 2, 0, nc.gpsimd)
+                blend_finish_half(UNITS - 2, 1, nc.vector)
+                store_half(UNITS - 2, 1)
+                store_half(UNITS - 2, 0)
+        for step in range(2):
+            for b in range(HALVES):
+                blend_step(UNITS - 1, b, step, nc.vector)
+        for b in range(HALVES):
+            store_half(UNITS - 1, b)

@@ -53,19 +53,21 @@ def tile_blockdiagonalgru_e_kernel(
         nc.gpsimd.memset(warm[:], 0.0)
         nc.scalar.activation(out=warm[:], in_=warm[:], func=ACT.Sigmoid)
 
-        ident = keep.tile([P, P], F32, name="ident")
-        make_identity(nc, ident[:])
-
         z_rows = keep.tile([P, HID], BF16, name="z_rows")
         bias_rows = keep.tile([P, 2, P], BF16, name="bias_rows")
+        runs = BLOCKS * GATES * TILES
+        for m, b in enumerate((b_ih, b_hh)):
+            small_queue.dma_start(out=bias_rows[0:runs, m, :], in_=b.rearrange("g (c q) -> (g c) q", q=P))
+        ident = keep.tile([P, P], F32, name="ident")
+        make_identity(nc, ident[:])
 
         plane_tiles = []
         for a in range(BLOCKS // PLANES):
             planes = keep.tile([P, 2, GATE_COLS], U8, name="planes%d" % a, align_bytes=64)
             plane_tiles.append(planes)
-        nc.vector.memset(bias_rows[:], 0.0)
-        nc.vector.memset(plane_tiles[0][:].rearrange("p m n -> p (m n)").bitcast(I32), 0)
         nc.vector.memset(z_rows[:], 0.0)
+        nc.vector.memset(plane_tiles[0][:].rearrange("p m n -> p (m n)").bitcast(I32), 0)
+        nc.vector.memset(bias_rows[runs:P, :, :], 0.0)
         nc.vector.memset(plane_tiles[1][:].rearrange("p m n -> p (m n)").bitcast(I32), 0)
 
         def load_planes(a, m):
@@ -102,11 +104,8 @@ def tile_blockdiagonalgru_e_kernel(
                     in_=dram_side.rearrange(split, gate=GATES, piece=pieces)[:, :, piece, :],
                 )
 
-        runs = BLOCKS * GATES * TILES
         for m, b in enumerate((b_ih, b_hh)):
-            small_queue.dma_start(out=bias_rows[0:runs, m, :], in_=b.rearrange("g (c q) -> (g c) q", q=P))
-        for m, b in enumerate((b_ih, b_hh)):
-            small_queue.dma_start(out=z_rows[m * BLOCKS : (m + 1) * BLOCKS, :], in_=b[:, Z * HID : (Z + 1) * HID])
+            nc.sync.dma_start(out=z_rows[m * BLOCKS : (m + 1) * BLOCKS, :], in_=b[:, Z * HID : (Z + 1) * HID])
         load_planes(0, 0)
         load_part(0)
         load_part(1)
@@ -155,14 +154,17 @@ def tile_blockdiagonalgru_e_kernel(
         z_bias = keep.tile([P, BLOCKS, HID], F32, name="z_bias")
         z_bias_ps = {}
 
-        def spread_z_bias(g):
-            z_bias_ps[g] = spare_tile([P, HID], "z_bias_ps%d" % g)
+        def spread_z_bias(g, tag=None):
+            if tag is None:
+                z_bias_ps[g] = spare_tile([P, HID], "z_bias_ps%d" % g)
+            else:
+                z_bias_ps[g] = psum.tile([P, HID], F32, name="z_bias_ps%d" % g, tag=tag)
             nc.tensor.matmul(
                 out=z_bias_ps[g][:], lhsT=pick[:, g : g + 1].to_broadcast([P, P]), rhs=z_rows[:], start=True, stop=True
             )
 
-        def copy_z_bias(g):
-            if g > 0:
+        def copy_z_bias(g, scalar):
+            if scalar:
                 nc.scalar.copy(out=z_bias[:, g, :], in_=z_bias_ps[g][:])
             else:
                 nc.vector.tensor_copy(out=z_bias[:, g, :], in_=z_bias_ps[g][:])
@@ -342,23 +344,31 @@ def tile_blockdiagonalgru_e_kernel(
             cols = slice(s * UNIT_COLS, (s + 1) * UNIT_COLS)
             nc.sync.dma_start(out=out[b * P : (b + 1) * P, cols], in_=out_tiles[s][:, b, :])
 
+        for g in range(len(SUMS)):
+            spread_z_bias(g, SUMS[g])
+        for g in range(len(SUMS)):
+            copy_z_bias(g, g % 2 == 0)
         transpose_part(0)
         transpose_part(1)
+        nc.vector.tensor_copy(out=bias_rows32[:], in_=bias_rows[:])
+        transpose_biases()
         copy_part(0)
         quantise(0, 0)
         copy_part(1)
-        quantise(0, 1)
-        nc.vector.tensor_copy(out=bias_rows32[:], in_=bias_rows[:])
-        transpose_biases()
         finish_biases()
+        quantise(0, 1)
+        for g in range(len(SUMS), BLOCKS):
+            spread_z_bias(g)
+        copy_z_bias(4, True)
+        copy_z_bias(5, True)
+        copy_z_bias(6, False)
+        copy_z_bias(7, False)
 
         for s in range(UNITS + 2):
             for q in parts_of_turn(s - 1):
                 copy_part(q)
             if s < UNITS:
                 multiply(s)
-            if s == 0:
-                spread_z_bias(0)
             if s >= 2:
                 blend_difference(s - 2)
             for q in parts_of_turn(s - 1):
@@ -370,16 +380,10 @@ def tile_blockdiagonalgru_e_kernel(
             if 1 <= s <= UNITS:
                 candidate(s - 1)
                 update_gate(s - 1)
-            if s % 2 == 1 and (s + 1) // 2 < BLOCKS:
-                copy_z_bias((s + 1) // 2)
             for q in parts_of_turn(s):
                 transpose_part(q)
-            if s % 2 == 0 and s // 2 + 1 < BLOCKS:
-                spread_z_bias(s // 2 + 1)
             if 1 <= s <= UNITS:
                 turn_back(s - 1)
-            if s == 0:
-                copy_z_bias(0)
             if s < UNITS:
                 add_z_bias(s)
                 add_in(s)

@@ -391,8 +391,9 @@ def tile_blockdiagonalgru_e_kernel(
                 blend_finish(s - 2)
                 store(s - 2)
             if s == UNITS:
-                blend_finish_half(UNITS - 2, 0, nc.gpsimd)
-                blend_finish_half(UNITS - 2, 1, nc.vector)
+                for step in range(2):
+                    for b in range(HALVES):
+                        blend_step(UNITS - 2, b, step, nc.vector)
                 store_half(UNITS - 2, 1)
                 store_half(UNITS - 2, 0)
         for step in range(2):

@@ -307,8 +307,8 @@ def tile_blockdiagonalgru_e_kernel(
 
         def turn_back(s):
             ps = spare_tile([P, HALVES, PAIR, P], "c_back%d" % s)
-            for b in range(HALVES):
-                for i in range(PAIR):
+            for i in range(PAIR):
+                for b in range(HALVES):
                     nc.tensor.transpose(ps[:, b, i, :], gate_tiles[s]["c"][:, i, b * P : (b + 1) * P], ident[:])
             back_ps[s] = ps
 

@@ -78,12 +78,19 @@ def tile_blockdiagonalgru_e_kernel(
                         in_=scales[PLANES * a : PLANES * (a + 1), 4 * quad : 4 * quad + 4, :].bitcast(I32),
                     )
 
-        part_tiles = [keep.tile([P, HALVES, K], BF16, name="part%d" % q) for q in range(PARTS)]
+        first_tiles = [keep.tile([P, HALVES, 2 * K], BF16, name="first%d" % m) for m in range(2)]
+        part_tiles = [first_tiles[q % 2][:, :, K * (q // 2) : K * (q // 2 + 1)] for q in range(4)]
+        for q in range(4, PARTS):
+            later = keep.tile([P, HALVES, K], BF16, name="part%d" % q)
+            part_tiles.append(later[:])
+
+        def load_first(m):
+            nc.sync.dma_start(out=first_tiles[m][:], in_=(x, h)[m].rearrange("(b p) c -> p b c", p=P)[:, :, 0 : 2 * K])
 
         def load_part(q):
             src = (x, h)[q % 2]
             cols = slice(K * (q // 2), K * (q // 2 + 1))
-            nc.sync.dma_start(out=part_tiles[q][:], in_=src.rearrange("(b p) c -> p b c", p=P)[:, :, cols])
+            nc.sync.dma_start(out=part_tiles[q], in_=src.rearrange("(b p) c -> p b c", p=P)[:, :, cols])
 
         word_tiles = [
             [keep.tile([P, GATE_COLS], U32, name="w%d_%d" % (m, g), align_bytes=64) for g in range(BLOCKS)]
@@ -107,8 +114,8 @@ def tile_blockdiagonalgru_e_kernel(
         for m, b in enumerate((b_ih, b_hh)):
             nc.sync.dma_start(out=z_rows[m * BLOCKS : (m + 1) * BLOCKS, :], in_=b[:, Z * HID : (Z + 1) * HID])
         load_planes(0, 0)
-        load_part(0)
-        load_part(1)
+        load_first(0)
+        load_first(1)
         load_words(0)
         load_planes(0, 1)
         load_words(1)
@@ -119,7 +126,8 @@ def tile_blockdiagonalgru_e_kernel(
             if s > 1:
                 load_words(s)
             for q in parts_of_turn(s):
-                load_part(q)
+                if q >= 4:
+                    load_part(q)
 
         pick = keep.tile([P, BLOCKS], BF16, name="pick")
         nc.vector.tensor_tensor(out=pick[:], in0=ident[:, 0:BLOCKS], in1=ident[:, BLOCKS : 2 * BLOCKS], op=ALU.add)
@@ -139,7 +147,7 @@ def tile_blockdiagonalgru_e_kernel(
         bias_ps = {}
 
         def transpose_biases():
-            bias_ps[0] = spare_tile([P, 2, P], "bias_ps")
+            bias_ps[0] = psum.tile([P, 2, P], F32, name="bias_ps", tag=SUMS[-1])
             for m in range(2):
                 nc.tensor.transpose(bias_ps[0][:, m, :], bias_rows32[:, m, :], ident[:])
 
@@ -349,7 +357,9 @@ def tile_blockdiagonalgru_e_kernel(
         for g in range(len(SUMS)):
             copy_z_bias(g, g % 2 == 0)
         transpose_part(0)
+        transpose_part(2)
         transpose_part(1)
+        transpose_part(3)
         nc.vector.tensor_copy(out=bias_rows32[:], in_=bias_rows[:])
         transpose_biases()
         copy_part(0)
@@ -358,10 +368,10 @@ def tile_blockdiagonalgru_e_kernel(
         finish_biases()
         quantise(0, 1)
         for g in range(len(SUMS), BLOCKS):
-            spread_z_bias(g)
+            spread_z_bias(g, SUMS[g - len(SUMS)])
         copy_z_bias(4, True)
-        copy_z_bias(5, True)
-        copy_z_bias(6, False)
+        copy_z_bias(5, False)
+        copy_z_bias(6, True)
         copy_z_bias(7, False)
 
         for s in range(UNITS + 2):
@@ -381,7 +391,8 @@ def tile_blockdiagonalgru_e_kernel(
                 candidate(s - 1)
                 update_gate(s - 1)
             for q in parts_of_turn(s):
-                transpose_part(q)
+                if q >= 4:
+                    transpose_part(q)
             if 1 <= s <= UNITS:
                 turn_back(s - 1)
             if s < UNITS:

@@ -56,27 +56,31 @@ def tile_blockdiagonalgru_e_kernel(
         z_rows = keep.tile([P, HID], BF16, name="z_rows")
         bias_rows = keep.tile([P, 2, P], BF16, name="bias_rows")
         runs = BLOCKS * GATES * TILES
-        for m, b in enumerate((b_ih, b_hh)):
-            small_queue.dma_start(out=bias_rows[0:runs, m, :], in_=b.rearrange("g (c q) -> (g c) q", q=P))
         ident = keep.tile([P, P], F32, name="ident")
         make_identity(nc, ident[:])
+        for m, b in enumerate((b_ih, b_hh)):
+            small_queue.dma_start(out=bias_rows[0:runs, m, :], in_=b.rearrange("g (c q) -> (g c) q", q=P))
 
         plane_tiles = []
         for a in range(BLOCKS // PLANES):
             planes = keep.tile([P, 2, GATE_COLS], U8, name="planes%d" % a, align_bytes=64)
             plane_tiles.append(planes)
-        nc.vector.memset(z_rows[:], 0.0)
-        nc.vector.memset(plane_tiles[0][:].rearrange("p m n -> p (m n)").bitcast(I32), 0)
         nc.vector.memset(bias_rows[runs:P, :, :], 0.0)
         nc.vector.memset(plane_tiles[1][:].rearrange("p m n -> p (m n)").bitcast(I32), 0)
 
         def load_planes(a, m):
             for scales in ((W_ih_scales, W_hh_scales)[m],):
                 for quad in range(4):
-                    nc.sync.dma_start(
-                        out=plane_tiles[a][32 * quad : 32 * quad + 4 * PLANES, m, :].bitcast(I32),
-                        in_=scales[PLANES * a : PLANES * (a + 1), 4 * quad : 4 * quad + 4, :].bitcast(I32),
-                    )
+                    if a == 0:
+                        nc.sync.dma_start(
+                            out=plane_tiles[a][32 * quad : 32 * (quad + 1), m, :].bitcast(I32),
+                            in_=scales[:, 4 * quad : 4 * quad + 4, :].bitcast(I32),
+                        )
+                    else:
+                        nc.sync.dma_start(
+                            out=plane_tiles[a][32 * quad : 32 * quad + 4 * PLANES, m, :].bitcast(I32),
+                            in_=scales[PLANES * a : PLANES * (a + 1), 4 * quad : 4 * quad + 4, :].bitcast(I32),
+                        )
 
         first_tiles = [keep.tile([P, HALVES, 2 * K], BF16, name="first%d" % m) for m in range(2)]
         part_tiles = [first_tiles[q % 2][:, :, K * (q // 2) : K * (q // 2 + 1)] for q in range(4)]
@@ -112,7 +116,10 @@ def tile_blockdiagonalgru_e_kernel(
                 )
 
         for m, b in enumerate((b_ih, b_hh)):
-            nc.sync.dma_start(out=z_rows[m * BLOCKS : (m + 1) * BLOCKS, :], in_=b[:, Z * HID : (Z + 1) * HID])
+            nc.sync.dma_start(
+                out=z_rows[m * (P // 2) : (m + 1) * (P // 2), :],
+                in_=b[:, Z * HID : (Z + 1) * HID].partition_broadcast(P // 2 // BLOCKS),
+            )
         load_planes(0, 0)
         load_first(0)
         load_first(1)
@@ -130,7 +137,7 @@ def tile_blockdiagonalgru_e_kernel(
                     load_part(q)
 
         pick = keep.tile([P, BLOCKS], BF16, name="pick")
-        nc.vector.tensor_tensor(out=pick[:], in0=ident[:, 0:BLOCKS], in1=ident[:, BLOCKS : 2 * BLOCKS], op=ALU.add)
+        nc.vector.tensor_tensor(out=pick[:], in0=ident[:, 0:BLOCKS], in1=ident[:, P // 2 : P // 2 + BLOCKS], op=ALU.add)
 
         bias_rows32 = keep.tile([P, 2, P], F32, name="bias_rows32")
 
@@ -147,7 +154,7 @@ def tile_blockdiagonalgru_e_kernel(
         bias_ps = {}
 
         def transpose_biases():
-            bias_ps[0] = psum.tile([P, 2, P], F32, name="bias_ps", tag=SUMS[-1])
+            bias_ps[0] = psum.tile([P, 2, P], F32, name="bias_ps", tag=SUMS[0])
             for m in range(2):
                 nc.tensor.transpose(bias_ps[0][:, m, :], bias_rows32[:, m, :], ident[:])
 
@@ -352,9 +359,12 @@ def tile_blockdiagonalgru_e_kernel(
             cols = slice(s * UNIT_COLS, (s + 1) * UNIT_COLS)
             nc.sync.dma_start(out=out[b * P : (b + 1) * P, cols], in_=out_tiles[s][:, b, :])
 
-        for g in range(len(SUMS)):
-            spread_z_bias(g, SUMS[g])
-        for g in range(len(SUMS)):
+        for g in range(BLOCKS - 2):
+            if g < spare_banks:
+                spread_z_bias(g)
+            else:
+                spread_z_bias(g, SUMS[g - spare_banks])
+        for g in range(BLOCKS - 2):
             copy_z_bias(g, g % 2 == 0)
         transpose_part(0)
         transpose_part(2)
@@ -367,12 +377,10 @@ def tile_blockdiagonalgru_e_kernel(
         copy_part(1)
         finish_biases()
         quantise(0, 1)
-        for g in range(len(SUMS), BLOCKS):
-            spread_z_bias(g, SUMS[g - len(SUMS)])
-        copy_z_bias(4, True)
-        copy_z_bias(5, False)
-        copy_z_bias(6, True)
-        copy_z_bias(7, False)
+        spread_z_bias(BLOCKS - 2, SUMS[-2])
+        spread_z_bias(BLOCKS - 1, SUMS[-1])
+        copy_z_bias(BLOCKS - 2, True)
+        copy_z_bias(BLOCKS - 1, False)
 
         for s in range(UNITS + 2):
             for q in parts_of_turn(s - 1):

@@ -65,22 +65,17 @@ def tile_blockdiagonalgru_e_kernel(
         for a in range(BLOCKS // PLANES):
             planes = keep.tile([P, 2, GATE_COLS], U8, name="planes%d" % a, align_bytes=64)
             plane_tiles.append(planes)
+        nc.vector.memset(plane_tiles[0][:].rearrange("p m n -> p (m n)").bitcast(I32), 0)
         nc.vector.memset(bias_rows[runs:P, :, :], 0.0)
         nc.vector.memset(plane_tiles[1][:].rearrange("p m n -> p (m n)").bitcast(I32), 0)
 
         def load_planes(a, m):
             for scales in ((W_ih_scales, W_hh_scales)[m],):
                 for quad in range(4):
-                    if a == 0:
-                        nc.sync.dma_start(
-                            out=plane_tiles[a][32 * quad : 32 * (quad + 1), m, :].bitcast(I32),
-                            in_=scales[:, 4 * quad : 4 * quad + 4, :].bitcast(I32),
-                        )
-                    else:
-                        nc.sync.dma_start(
-                            out=plane_tiles[a][32 * quad : 32 * quad + 4 * PLANES, m, :].bitcast(I32),
-                            in_=scales[PLANES * a : PLANES * (a + 1), 4 * quad : 4 * quad + 4, :].bitcast(I32),
-                        )
+                    nc.sync.dma_start(
+                        out=plane_tiles[a][32 * quad : 32 * quad + 4 * PLANES, m, :].bitcast(I32),
+                        in_=scales[PLANES * a : PLANES * (a + 1), 4 * quad : 4 * quad + 4, :].bitcast(I32),
+                    )
 
         first_tiles = [keep.tile([P, HALVES, 2 * K], BF16, name="first%d" % m) for m in range(2)]
         part_tiles = [first_tiles[q % 2][:, :, K * (q // 2) : K * (q // 2 + 1)] for q in range(4)]
@@ -103,7 +98,7 @@ def tile_blockdiagonalgru_e_kernel(
 
         def load_words(s):
             g, piece = s // UNITS_PER_BLOCK, s % UNITS_PER_BLOCK
-            pieces = UNITS_PER_BLOCK if g == 0 else 1
+            pieces = UNITS_PER_BLOCK if g <= 1 else 1
             if piece >= pieces:
                 return
             split = "p (gate piece c) -> p gate piece c"
@@ -120,17 +115,18 @@ def tile_blockdiagonalgru_e_kernel(
                 out=z_rows[m * (P // 2) : (m + 1) * (P // 2), :],
                 in_=b[:, Z * HID : (Z + 1) * HID].partition_broadcast(P // 2 // BLOCKS),
             )
-        load_planes(0, 0)
         load_first(0)
         load_first(1)
+        load_planes(0, 0)
         load_words(0)
         load_planes(0, 1)
         load_words(1)
+        load_words(2)
         for s in range(UNITS):
             if s == PLANES * UNITS_PER_BLOCK:
                 load_planes(1, 0)
                 load_planes(1, 1)
-            if s > 1:
+            if s > 2:
                 load_words(s)
             for q in parts_of_turn(s):
                 if q >= 4:

from contextlib import ExitStack

import concourse.mybir as mybir
from concourse.masks import make_identity

F32 = mybir.dt.float32
BF16 = mybir.dt.bfloat16
I32 = mybir.dt.int32
U32 = mybir.dt.uint32
U8 = mybir.dt.uint8
FP8X4 = mybir.dt.float8_e4m3fn_x4
ALU = mybir.AluOpType
ACT = mybir.ActivationFunctionType

P = 128
BATCH = 256
HALVES = BATCH // P
BLOCKS = 8
K = 512
HID = 512
GATES = 3
GATE_COLS = GATES * HID
TILES = HID // P
PAIR = 2
UNITS = BLOCKS * TILES // PAIR
UNITS_PER_BLOCK = TILES // PAIR
UNIT_COLS = PAIR * P
PARTS = 2 * BLOCKS
PLANES = 4
AHEAD = 3
R, Z, N = 0, 1, 2
SUMS = ("r", "hn", "z", "in")

FLOPS = 2 * BATCH * K * GATE_COLS * 2 * BLOCKS


def parts_of_turn(s):
    return [q for q in range(2, PARTS) if max(q - AHEAD, 0) == s]


def tile_blockdiagonalgru_e_kernel(
    tc, x, h, W_ih_words, W_ih_scales, W_hh_words, W_hh_scales, b_ih, b_hh, out
):
    nc = tc.nc
    small_queue = nc.gpsimd
    with ExitStack() as ctx:
        ctx.enter_context(tc.manual_schedule())
        keep = ctx.enter_context(tc.tile_pool(name="keep", bufs=1))
        work = ctx.enter_context(tc.tile_pool(name="work", bufs=2))
        psum = ctx.enter_context(tc.psum_pool(name="psum", bufs=1))

        warm = keep.tile([P, 1], F32, name="warm")
        nc.gpsimd.memset(warm[:], 0.0)
        nc.scalar.activation(out=warm[:], in_=warm[:], func=ACT.Sigmoid)

        z_rows = keep.tile([P, HID], BF16, name="z_rows")
        bias_rows = keep.tile([P, 2, P], BF16, name="bias_rows")
        runs = BLOCKS * GATES * TILES
        ident = keep.tile([P, P], F32, name="ident")
        make_identity(nc, ident[:])
        for m, b in enumerate((b_ih, b_hh)):
            small_queue.dma_start(out=bias_rows[0:runs, m, :], in_=b.rearrange("g (c q) -> (g c) q", q=P))

        plane_tiles = []
        for a in range(BLOCKS // PLANES):
            planes = keep.tile([P, 2, GATE_COLS], U8, name="planes%d" % a, align_bytes=64)
            plane_tiles.append(planes)
        nc.vector.memset(plane_tiles[0][:].rearrange("p m n -> p (m n)").bitcast(I32), 0)
        nc.vector.memset(bias_rows[runs:P, :, :], 0.0)
        nc.vector.memset(plane_tiles[1][:].rearrange("p m n -> p (m n)").bitcast(I32), 0)

        def load_planes(a, m):
            for scales in ((W_ih_scales, W_hh_scales)[m],):
                for quad in range(4):
                    nc.sync.dma_start(
                        out=plane_tiles[a][32 * quad : 32 * quad + 4 * PLANES, m, :].bitcast(I32),
                        in_=scales[PLANES * a : PLANES * (a + 1), 4 * quad : 4 * quad + 4, :].bitcast(I32),
                    )

        first_tiles = [keep.tile([P, HALVES, 2 * K], BF16, name="first%d" % m) for m in range(2)]
        part_tiles = [first_tiles[q % 2][:, :, K * (q // 2) : K * (q // 2 + 1)] for q in range(4)]
        for q in range(4, PARTS):
            later = keep.tile([P, HALVES, K], BF16, name="part%d" % q)
            part_tiles.append(later[:])

        def load_first(m):
            nc.sync.dma_start(out=first_tiles[m][:], in_=(x, h)[m].rearrange("(b p) c -> p b c", p=P)[:, :, 0 : 2 * K])

        def load_part(q):
            src = (x, h)[q % 2]
            cols = slice(K * (q // 2), K * (q // 2 + 1))
            nc.sync.dma_start(out=part_tiles[q], in_=src.rearrange("(b p) c -> p b c", p=P)[:, :, cols])

        word_tiles = [
            [keep.tile([P, GATE_COLS], U32, name="w%d_%d" % (m, g), align_bytes=64) for g in range(BLOCKS)]
            for m in range(2)
        ]

        def load_words(s):
            g, piece = s // UNITS_PER_BLOCK, s % UNITS_PER_BLOCK
            pieces = UNITS_PER_BLOCK if g <= 1 else 1
            if piece >= pieces:
                return
            split = "p (gate piece c) -> p gate piece c"
            for m, words in enumerate((W_ih_words, W_hh_words)):
                sbuf_side = word_tiles[m][g][:].bitcast(I32)
                dram_side = words[g].rearrange("p n t -> p (n t)").bitcast(I32)
                nc.sync.dma_start(
                    out=sbuf_side.rearrange(split, gate=GATES, piece=pieces)[:, :, piece, :],
                    in_=dram_side.rearrange(split, gate=GATES, piece=pieces)[:, :, piece, :],
                )

        for m, b in enumerate((b_ih, b_hh)):
            nc.sync.dma_start(
                out=z_rows[m * (P // 2) : (m + 1) * (P // 2), :],
                in_=b[:, Z * HID : (Z + 1) * HID].partition_broadcast(P // 2 // BLOCKS),
            )
        load_first(0)
        load_first(1)
        load_planes(0, 0)
        load_words(0)
        load_planes(0, 1)
        load_words(1)
        load_words(2)
        for s in range(UNITS):
            if s == PLANES * UNITS_PER_BLOCK:
                load_planes(1, 0)
                load_planes(1, 1)
            if s > 2:
                load_words(s)
            for q in parts_of_turn(s):
                if q >= 4:
                    load_part(q)

        pick = keep.tile([P, BLOCKS], BF16, name="pick")
        nc.vector.tensor_tensor(out=pick[:], in0=ident[:, 0:BLOCKS], in1=ident[:, P // 2 : P // 2 + BLOCKS], op=ALU.add)

        bias_rows32 = keep.tile([P, 2, P], F32, name="bias_rows32")

        spare_banks = 4
        spare_names = []

        def spare_tile(shape, name):
            t = psum.tile(shape, F32, name=name, tag="spare%d" % (len(spare_names) % spare_banks))
            spare_names.append(name)
            return t

        bias = keep.tile([P, 2, P], F32, name="bias")
        bias_sum = keep.tile([P, P], F32, name="bias_sum")
        bias_ps = {}

        def transpose_biases():
            bias_ps[0] = psum.tile([P, 2, P], F32, name="bias_ps", tag=SUMS[0])
            for m in range(2):
                nc.tensor.transpose(bias_ps[0][:, m, :], bias_rows32[:, m, :], ident[:])

        def finish_biases():
            nc.vector.tensor_copy(out=bias[:], in_=bias_ps[0][:])
            nc.vector.tensor_tensor(out=bias_sum[:], in0=bias[:, 0, :], in1=bias[:, 1, :], op=ALU.add)

        def bias_col(g, gate, j):
            col = (g * GATES + gate) * TILES + j
            return slice(col, col + 1)

        z_bias = keep.tile([P, BLOCKS, HID], F32, name="z_bias")
        z_bias_ps = {}

        def spread_z_bias(g, tag=None):
            if tag is None:
                z_bias_ps[g] = spare_tile([P, HID], "z_bias_ps%d" % g)
            else:
                z_bias_ps[g] = psum.tile([P, HID], F32, name="z_bias_ps%d" % g, tag=tag)
            nc.tensor.matmul(
                out=z_bias_ps[g][:], lhsT=pick[:, g : g + 1].to_broadcast([P, P]), rhs=z_rows[:], start=True, stop=True
            )

        def copy_z_bias(g, scalar):
            if scalar:
                nc.scalar.copy(out=z_bias[:, g, :], in_=z_bias_ps[g][:])
            else:
                nc.vector.tensor_copy(out=z_bias[:, g, :], in_=z_bias_ps[g][:])

        part_ps = {}
        grouped_tiles = {}
        code_tiles = {}

        def transpose_part(q):
            ps = spare_tile([P, 2, HALVES, P], "part_ps%d" % q)
            for u in range(2):
                for b in range(HALVES):
                    words = part_tiles[q][:, b, :].bitcast(F32)
                    nc.tensor.transpose(ps[:, u, b, :], words[:, u : K // 2 : 2], ident[:])
            part_ps[q] = ps

        def copy_part(q):
            g, operand = q // 2, q % 2
            if operand == 0:
                grouped_tiles[g] = work.tile(
                    [P, 2, BATCH * 4], BF16, name="grouped%d" % g, tag="grouped", align_bytes=64
                )
            nc.scalar.copy(
                out=grouped_tiles[g][:, operand, :].bitcast(F32).rearrange("p (n u) -> p n u", u=2),
                in_=part_ps[q][:].rearrange("p u b n -> p (b n) u"),
            )

        def quantise(g, operand=None):
            if operand != 1:
                codes = work.tile([P, 2, BATCH], U32, name="codes%d" % g, tag="codes", bufs=3, align_bytes=64)
                scales = work.tile([P, 2, BATCH], U8, name="scales%d" % g, tag="scales", bufs=3, align_bytes=64)
                code_tiles[g] = (codes, scales)
            codes, scales = code_tiles[g]
            if operand is None:
                nc.vector.quantize_mx(
                    out=codes[:].rearrange("p o n -> p (o n)").bitcast(FP8X4),
                    scales=scales[:].rearrange("p o n -> p (o n)"),
                    in_=grouped_tiles[g][:].rearrange("p o n -> p (o n)"),
                )
            else:
                nc.vector.quantize_mx(
                    out=codes[:, operand, :].bitcast(FP8X4), scales=scales[:, operand, :], in_=grouped_tiles[g][:, operand, :]
                )

        def weights(g, m, cols):
            offset = 4 * (g % PLANES)
            return word_tiles[m][g][:, cols].bitcast(FP8X4), plane_tiles[g // PLANES][offset:P, m, cols]

        def activations(g, m, rows):
            codes, scales = code_tiles[g]
            return codes[:, m, rows].bitcast(FP8X4), scales[:, m, rows]

        def columns_by_batch(acc, g, m, gate, j, start, stop):
            w, w_scale = weights(g, m, slice(gate * HID + j * P, gate * HID + (j + 1) * P))
            a, a_scale = activations(g, m, slice(0, BATCH))
            nc.tensor.matmul_mx(out=acc, lhsT=w, lhsT_scale=w_scale, rhs=a, rhs_scale=a_scale, start=start, stop=stop)

        def batch_by_columns(acc, g, m, gate, first, b, start, stop):
            w, w_scale = weights(g, m, slice(gate * HID + first, gate * HID + first + UNIT_COLS))
            a, a_scale = activations(g, m, slice(b * P, (b + 1) * P))
            nc.tensor.matmul_mx(out=acc, lhsT=a, lhsT_scale=a_scale, rhs=w, rhs_scale=w_scale, start=start, stop=stop)

        sums = {}
        gate_tiles = {}
        back_ps = {}
        out_tiles = [keep.tile([P, HALVES, UNIT_COLS], F32, name="new_h%d" % s) for s in range(UNITS)]

        def column_tiles(s):
            g = s // UNITS_PER_BLOCK
            return g, [PAIR * (s % UNITS_PER_BLOCK) + i for i in range(PAIR)]

        def multiply(s):
            g, tiles = column_tiles(s)
            acc = {}
            for name in SUMS:
                acc[name] = psum.tile([P, PAIR, BATCH], F32, name="%s_ps%d" % (name, s), tag=name)
            for i, j in enumerate(tiles):
                columns_by_batch(acc["r"][:, i, :], g, 0, R, j, True, False)
                columns_by_batch(acc["r"][:, i, :], g, 1, R, j, False, True)
            for i, j in enumerate(tiles):
                columns_by_batch(acc["hn"][:, i, :], g, 1, N, j, True, True)
            for b in range(HALVES):
                batch_by_columns(acc["z"][:, b, :], g, 0, Z, tiles[0] * P, b, True, False)
                batch_by_columns(acc["z"][:, b, :], g, 1, Z, tiles[0] * P, b, False, True)
            for i, j in enumerate(tiles):
                columns_by_batch(acc["in"][:, i, :], g, 0, N, j, True, True)
            sums[s] = acc
            gate_tiles[s] = {}
            for name, bufs in (("r", 2), ("t", 3), ("c", 2), ("zc", 4)):
                gate_tiles[s][name] = work.tile([P, PAIR, BATCH], F32, name="%s%d" % (name, s), tag=name, bufs=bufs)

        def reset_gate(s):
            g, tiles = column_tiles(s)
            for i, j in enumerate(tiles):
                nc.scalar.activation(
                    out=gate_tiles[s]["r"][:, i, :],
                    in_=sums[s]["r"][:, i, :],
                    func=ACT.Sigmoid,
                    bias=bias_sum[:, bias_col(g, R, j)],
                    scale=1.0,
                )

        def reset_times_hn(s):
            g, tiles = column_tiles(s)
            for i, j in enumerate(tiles):
                nc.vector.scalar_tensor_tensor(
                    out=gate_tiles[s]["t"][:, i, :],
                    in0=sums[s]["hn"][:, i, :],
                    scalar=bias[:, 1, bias_col(g, N, j)],
                    in1=gate_tiles[s]["r"][:, i, :],
                    op0=ALU.add,
                    op1=ALU.mult,
                )

        def add_in(s):
            t = gate_tiles[s]["t"]
            nc.vector.tensor_tensor(out=t[:], in0=t[:], in1=sums[s]["in"][:], op=ALU.add)

        def add_z_bias(s):
            g, tiles = column_tiles(s)
            both_halves = z_bias[:, g, tiles[0] * P : tiles[0] * P + UNIT_COLS].unsqueeze(1).to_broadcast(
                [P, HALVES, UNIT_COLS]
            )
            nc.vector.tensor_tensor(out=gate_tiles[s]["zc"][:], in0=sums[s]["z"][:], in1=both_halves, op=ALU.add)

        def update_gate(s):
            zc = gate_tiles[s]["zc"]
            nc.scalar.activation(out=zc[:], in_=zc[:], func=ACT.Sigmoid, scale=-1.0)

        def candidate(s):
            g, tiles = column_tiles(s)
            for i, j in enumerate(tiles):
                nc.scalar.activation(
                    out=gate_tiles[s]["c"][:, i, :],
                    in_=gate_tiles[s]["t"][:, i, :],
                    func=ACT.Tanh,
                    bias=bias[:, 0, bias_col(g, N, j)],
                    scale=1.0,
                )

        def turn_back(s):
            ps = spare_tile([P, HALVES, PAIR, P], "c_back%d" % s)
            for i in range(PAIR):
                for b in range(HALVES):
                    nc.tensor.transpose(ps[:, b, i, :], gate_tiles[s]["c"][:, i, b * P : (b + 1) * P], ident[:])
            back_ps[s] = ps

        def h_columns(s):
            first = (s % UNITS_PER_BLOCK) * UNIT_COLS
            return part_tiles[2 * (s // UNITS_PER_BLOCK) + 1][:, :, first : first + UNIT_COLS]

        def blend_difference(s):
            c_view = back_ps[s][:].rearrange("p b i q -> p b (i q)")
            nc.vector.tensor_tensor(out=out_tiles[s][:], in0=h_columns(s), in1=c_view, op=ALU.subtract)

        def blend_finish(s):
            o = out_tiles[s]
            nc.gpsimd.tensor_tensor(out=o[:], in0=gate_tiles[s]["zc"][:], in1=o[:], op=ALU.mult)
            nc.gpsimd.tensor_tensor(out=o[:], in0=h_columns(s), in1=o[:], op=ALU.subtract)

        def blend_step(s, b, step, engine):
            o = out_tiles[s][:, b, :]
            if step == 0:
                engine.tensor_tensor(out=o, in0=gate_tiles[s]["zc"][:, b, :], in1=o, op=ALU.mult)
            else:
                engine.tensor_tensor(out=o, in0=h_columns(s)[:, b, :], in1=o, op=ALU.subtract)

        def blend_finish_half(s, b, engine):
            for step in range(2):
                blend_step(s, b, step, engine)

        def store(s):
            cols = slice(s * UNIT_COLS, (s + 1) * UNIT_COLS)
            nc.sync.dma_start(out=out.rearrange("(b p) c -> p b c", p=P)[:, :, cols], in_=out_tiles[s][:])

        def store_half(s, b):
            cols = slice(s * UNIT_COLS, (s + 1) * UNIT_COLS)
            nc.sync.dma_start(out=out[b * P : (b + 1) * P, cols], in_=out_tiles[s][:, b, :])

        for g in range(BLOCKS - 2):
            if g < spare_banks:
                spread_z_bias(g)
            else:
                spread_z_bias(g, SUMS[g - spare_banks])
        for g in range(BLOCKS - 2):
            copy_z_bias(g, g % 2 == 0)
        transpose_part(0)
        transpose_part(2)
        transpose_part(1)
        transpose_part(3)
        nc.vector.tensor_copy(out=bias_rows32[:], in_=bias_rows[:])
        transpose_biases()
        copy_part(0)
        quantise(0, 0)
        copy_part(1)
        finish_biases()
        quantise(0, 1)
        spread_z_bias(BLOCKS - 2, SUMS[-2])
        spread_z_bias(BLOCKS - 1, SUMS[-1])
        copy_z_bias(BLOCKS - 2, True)
        copy_z_bias(BLOCKS - 1, False)

        for s in range(UNITS + 2):
            for q in parts_of_turn(s - 1):
                copy_part(q)
            if s < UNITS:
                multiply(s)
            if s >= 2:
                blend_difference(s - 2)
            for q in parts_of_turn(s - 1):
                if q % 2 == 1:
                    quantise(q // 2)
            if s < UNITS:
                reset_gate(s)
                reset_times_hn(s)
            if 1 <= s <= UNITS:
                candidate(s - 1)
                update_gate(s - 1)
            for q in parts_of_turn(s):
                if q >= 4:
                    transpose_part(q)
            if 1 <= s <= UNITS:
                turn_back(s - 1)
            if s < UNITS:
                add_z_bias(s)
                add_in(s)
            if 2 <= s < UNITS:
                blend_finish(s - 2)
                store(s - 2)
            if s == UNITS:
                for step in range(2):
                    for b in range(HALVES):
                        blend_step(UNITS - 2, b, step, nc.vector)
                store_half(UNITS - 2, 1)
                store_half(UNITS - 2, 0)
        for step in range(2):
            for b in range(HALVES):
                blend_step(UNITS - 1, b, step, nc.vector)
        for b in range(HALVES):
            store_half(UNITS - 1, b)
